import numpy as np
import ml_dtypes


def mxq(x, axis, fmt="e4m3"):
    dtype, down = {"e4m3": (ml_dtypes.float8_e4m3fn, 7), "e5m2": (ml_dtypes.float8_e5m2, 14)}[fmt]
    v = np.moveaxis(np.asarray(x, np.float32).astype(ml_dtypes.bfloat16).astype(np.float64), axis, -1)
    blocks = v.reshape(v.shape[:-1] + (-1, 32))
    amax = np.abs(blocks).max(-1, keepdims=True)
    byte = np.maximum(np.where(amax > 0, np.frexp(amax)[1] - 1 + 127, 0) - down, 1)
    scale = np.exp2(byte - 127.0)
    codes = (blocks / scale).astype(np.float32).astype(dtype).astype(np.float64)
    return np.moveaxis((codes * scale).reshape(v.shape), -1, axis)


WIDE = False


def mx_kscale(k):
    if not WIDE:
        return np.ones(k)
    levels = np.array([10, -10, 5, -5, 0])
    a = np.random.permutation(np.resize(levels, k // 512 * 4)).reshape(k // 512, 4)
    idx = np.arange(k)
    return np.exp2(a[idx // 512, idx % 128 // 32])


BF16 = ml_dtypes.bfloat16


def bf(x):
    return np.asarray(x, np.float32).astype(BF16)


def f64(x):
    return np.asarray(x).astype(np.float64)


B, H, K = 1024, 1024, 512
R = H ** -0.25


def setup_inputs():
    s = mx_kscale(H)
    return {
        "encoder_final_state": bf(np.random.standard_normal((B, H)) * s),
        "W_mu": bf(np.random.standard_normal((H, H)) * 0.55 * R / np.sqrt(H) / s[None, :]),
        "b_mu": bf(np.random.standard_normal(H) * 0.3 * R),
        "W_ls": bf(np.random.standard_normal((H, H)) * 0.5 / np.sqrt(H) / s[None, :]),
        "b_ls": bf(np.random.standard_normal(H) * 0.1),
        "mu_c": bf(np.random.standard_normal((K, H)) * 0.5 * R),
        "log_sigma_sq_c": bf(np.random.standard_normal((K, H)) * 0.4),
        "eps_z": bf(np.random.standard_normal((B, H)) * 0.55 * R),
    }


def reference(encoder_final_state, W_mu, b_mu, W_ls, b_ls, mu_c, log_sigma_sq_c, eps_z):
    xq = mxq(f64(encoder_final_state), 1, "e4m3")
    mu_z = (xq @ mxq(f64(W_mu), 1, "e4m3").T) + f64(b_mu)
    ls_z = (xq @ mxq(f64(W_ls), 1, "e4m3").T) + f64(b_ls)
    z = mu_z + np.exp(0.5 * ls_z) * f64(eps_z)
    inv_sig = np.exp(-f64(log_sigma_sq_c))
    mu_inv = f64(mu_c) * inv_sig
    c2 = np.sum(f64(mu_c) * mu_inv, axis=-1)
    d = (mxq(z * z, 1, "e4m3") @ mxq(inv_sig, 1, "e4m3").T) - 2.0 * (mxq(z, 1, "e4m3") @ mxq(mu_inv, 1, "e4m3").T) + c2[None, :]
    g = -d
    e = np.exp(g - g.max(-1, keepdims=True))
    att = e / e.sum(-1, keepdims=True)
    return z, att

@@ -1,0 +1,285 @@
+import concourse.mybir as mybir
+from concourse.masks import make_identity
+
+F32 = mybir.dt.float32
+BF16 = mybir.dt.bfloat16
+U32 = mybir.dt.uint32
+U8 = mybir.dt.uint8
+FP8X4 = mybir.dt.float8_e4m3fn_x4
+ACT = mybir.ActivationFunctionType
+ALU = mybir.AluOpType
+
+P = 128
+B, H, K = 1024, 1024, 512
+HALF = 512
+
+FLOPS = 2 * B * H * H * 2 + 2 * B * K * H * 2
+
+
+def quantise(nc, grouped, codes, scales):
+    nc.vector.quantize_mx(
+        out=codes.rearrange("p g c -> p (g c)").bitcast(FP8X4),
+        scales=scales.rearrange("p g c -> p (g c)"),
+        in_=grouped[:].rearrange("p g c t -> p (g c t)"),
+    )
+
+
+def rows_to_codes(nc, psum_tr, stage, ident, rows, codes, scales):
+    words = rows.bitcast(F32)
+    grouped = stage.tile([P, 2, HALF, 4], BF16, tag="grouped", align_bytes=64)
+    grouped_words = grouped[:].bitcast(F32)
+    for i in range(4):
+        bank = psum_tr.tile([P, 4, P], F32, tag="tr")
+        for j in range(4):
+            nc.tensor.transpose(bank[:, j, :], words[:, i, j * P : (j + 1) * P], ident[:])
+        copy_out = nc.scalar.copy if i % 2 == 0 else nc.vector.tensor_copy
+        copy_out(
+            out=grouped_words[:, :, i * P : (i + 1) * P, :],
+            in_=bank[:].rearrange("p (g u) r -> p g r u", g=2),
+        )
+    quantise(nc, grouped, codes, scales)
+
+
+def project(nc, bank, w_codes, w_scales, row_tile, x_codes, x_scales, bh):
+    half, i = divmod(row_tile, 4)
+    cols = slice(i * P, (i + 1) * P)
+    for g in range(2):
+        nc.tensor.matmul_mx(
+            out=bank[:],
+            lhsT=w_codes[:, half, g, cols].bitcast(FP8X4),
+            lhsT_scale=w_scales[:, half, g, cols],
+            rhs=x_codes[:, bh, g, :].bitcast(FP8X4),
+            rhs_scale=x_scales[:, bh, g, :],
+            start=(g == 0),
+            stop=(g == 1),
+        )
+
+
+def tile_latent_pa_kernel(
+    tc, encoder_final_state, W_mu, b_mu, W_ls, b_ls, mu_c, log_sigma_sq_c, eps_z, out_0, out_1
+):
+    nc = tc.nc
+    with tc.tile_pool(name="const", bufs=1) as const, tc.tile_pool(name="raw", bufs=1) as raw, tc.tile_pool(
+        name="codes", bufs=1
+    ) as keep, tc.tile_pool(name="stage", bufs=4) as stage, tc.psum_pool(name="psum_tr", bufs=3) as psum_tr, tc.psum_pool(
+        name="psum_mm", bufs=5
+    ) as psum_mm:
+        ident = const.tile([P, P], F32)
+        make_identity(nc, ident[:])
+        ones = const.tile([P, P], F32)
+        nc.vector.memset(ones[:], 1.0)
+        bias_rows = const.tile([P, P], F32)
+        nc.vector.memset(bias_rows[:], 0.0)
+        nc.sync.dma_start(out=bias_rows[0:4, :].bitcast(BF16), in_=b_mu.rearrange("(a w) -> a w", a=4))
+        nc.sync.dma_start(out=bias_rows[4:8, :].bitcast(BF16), in_=b_ls.rearrange("(a w) -> a w", a=4))
+
+        x_nat = raw.tile([P, 8, H], BF16)
+        wls_nat = raw.tile([P, 8, H], BF16)
+        wmu_nat = raw.tile([P, 8, H], BF16)
+        eps_nat = raw.tile([P, 8, H], BF16)
+
+        x_codes = keep.tile([P, 2, 2, HALF], U32, align_bytes=64)
+        x_scales = keep.tile([P, 2, 2, HALF], U8, align_bytes=64)
+        wls_codes = keep.tile([P, 2, 2, HALF], U32, align_bytes=64)
+        wls_scales = keep.tile([P, 2, 2, HALF], U8, align_bytes=64)
+        wmu_codes = keep.tile([P, 2, 2, HALF], U32, align_bytes=64)
+        wmu_scales = keep.tile([P, 2, 2, HALF], U8, align_bytes=64)
+        inv_codes = keep.tile([P, 2, K], U32, align_bytes=64)
+        inv_scales = keep.tile([P, 2, K], U8, align_bytes=64)
+        minv_codes = keep.tile([P, 2, K], U32, align_bytes=64)
+        minv_scales = keep.tile([P, 2, K], U8, align_bytes=64)
+        z_codes = keep.tile([P, 4, 2, HALF], U32, align_bytes=64)
+        z_scales = keep.tile([P, 4, 2, HALF], U8, align_bytes=64)
+        c2_all = const.tile([P, K], F32)
+        bias = const.tile([P, 16], F32)
+
+        with tc.tile_pool(name="cl_raw", bufs=1) as cl_raw, tc.tile_pool(name="cl_tmp", bufs=2) as cl_tmp:
+            ls_nat = cl_raw.tile([P, 4, H], BF16)
+            mu_nat = cl_raw.tile([P, 4, H], BF16)
+            for ch in range(2):
+                for nat, src in ((ls_nat, log_sigma_sq_c), (mu_nat, mu_c)):
+                    nc.sync.dma_start(
+                        out=nat[:, 2 * ch : 2 * ch + 2, :],
+                        in_=src[256 * ch : 256 * ch + 256, :].rearrange("(t r) h -> r t h", r=P),
+                    )
+            for half in range(2):
+                nc.sync.dma_start(
+                    out=x_nat[:, 4 * half : 4 * half + 4, :],
+                    in_=encoder_final_state[HALF * half : HALF * half + HALF, :].rearrange("(t r) h -> r t h", r=P),
+                )
+            for half in range(2):
+                for nat, src in ((wls_nat, W_ls), (wmu_nat, W_mu)):
+                    nc.sync.dma_start(
+                        out=nat[:, 4 * half : 4 * half + 4, :].rearrange("q (a e) h -> q a (e h)", e=2),
+                        in_=src[HALF * half : HALF * half + HALF, :].rearrange("(a q e) h -> q a (e h)", q=P, e=2),
+                    )
+            for half in range(2):
+                nc.sync.dma_start(
+                    out=eps_nat[:, 4 * half : 4 * half + 4, :],
+                    in_=eps_z[HALF * half : HALF * half + HALF, :].rearrange("(t r) h -> r t h", r=P),
+                )
+
+            ls_words = ls_nat[:].bitcast(F32)
+            mu_words = mu_nat[:].bitcast(F32)
+            inv_grouped = stage.tile([P, 2, K, 4], BF16, tag="grouped", align_bytes=64)
+            minv_grouped = stage.tile([P, 2, K, 4], BF16, tag="grouped", align_bytes=64)
+            prod = cl_raw.tile([P, 2, 4, K], F32)
+            for g in range(2):
+                for ch in range(2):
+                    cols = slice(256 * ch, 256 * ch + 256)
+                    ls_bank = psum_tr.tile([P, 2, 256], F32, tag="tr")
+                    mu_bank = psum_tr.tile([P, 2, 256], F32, tag="tr")
+                    for bank, words in ((ls_bank, ls_words), (mu_bank, mu_words)):
+                        for u in range(2):
+                            for j in range(2):
+                                nc.tensor.transpose(
+                                    bank[:, u, j * P : (j + 1) * P],
+                                    words[:, 2 * ch + j, (2 * g + u) * P : (2 * g + u + 1) * P],
+                                    ident[:],
+                                )
+                    ls_view = ls_bank[:].bitcast(BF16).rearrange("p u (c e) -> p c u e", e=2)
+                    mu_view = mu_bank[:].bitcast(BF16).rearrange("p u (c e) -> p c u e", e=2)
+                    inv32 = cl_tmp.tile([P, 256, 2, 2], F32)
+                    nc.scalar.activation(out=inv32[:], in_=ls_view, func=ACT.Exp, scale=-1.0)
+                    nc.scalar.activation(
+                        out=inv_grouped[:, g, cols, :].rearrange("p c (u e) -> p c u e", e=2),
+                        in_=ls_view,
+                        func=ACT.Exp,
+                        scale=-1.0,
+                    )
+                    minv32 = cl_tmp.tile([P, 256, 2, 2], F32)
+                    nc.vector.tensor_tensor(out=minv32[:], in0=mu_view, in1=inv32[:], op=ALU.mult)
+                    nc.scalar.activation(
+                        out=minv_grouped[:, g, cols, :].rearrange("p c (u e) -> p c u e", e=2),
+                        in_=minv32[:],
+                        func=ACT.Copy,
+                        scale=-2.0,
+                    )
+                    nc.vector.tensor_tensor(
+                        out=prod[:, g, :, cols].rearrange("p (u e) c -> p c u e", e=2),
+                        in0=mu_view,
+                        in1=minv32[:],
+                        op=ALU.mult,
+                    )
+            quantise(nc, inv_grouped, inv_codes[:], inv_scales[:])
+            quantise(nc, minv_grouped, minv_codes[:], minv_scales[:])
+            c2_bank = psum_mm.tile([P, K], F32, tag="mm")
+            for n in range(8):
+                nc.tensor.matmul(
+                    c2_bank[:], lhsT=ones[:], rhs=prod[:, n // 4, n % 4, :], start=(n == 0), stop=(n == 7)
+                )
+            nc.vector.tensor_copy(out=c2_all[:], in_=c2_bank[:])
+
+            bias_bank = psum_tr.tile([P, P], F32, tag="tr")
+            nc.tensor.transpose(bias_bank[:], bias_rows[:], ident[:])
+            nc.vector.tensor_copy(out=bias[:, 0:8], in_=bias_bank[:, 0:4].bitcast(BF16))
+            nc.vector.tensor_scalar(
+                out=bias[:, 8:16], in0=bias_bank[:, 4:8].bitcast(BF16), scalar1=0.5, scalar2=None, op0=ALU.mult
+            )
+
+        for half in range(2):
+            rows_to_codes(
+                nc, psum_tr, stage, ident, x_nat[:, 4 * half : 4 * half + 4, :], x_codes[:, half], x_scales[:, half]
+            )
+        for half in range(2):
+            rows_to_codes(
+                nc, psum_tr, stage, ident, wls_nat[:, 4 * half : 4 * half + 4, :], wls_codes[:, half], wls_scales[:, half]
+            )
+            rows_to_codes(
+                nc, psum_tr, stage, ident, wmu_nat[:, 4 * half : 4 * half + 4, :], wmu_codes[:, half], wmu_scales[:, half]
+            )
+
+        eps_words = eps_nat[:].bitcast(F32)
+        with tc.tile_pool(name="s1", bufs=2) as s1, tc.tile_pool(name="s2", bufs=2) as s2:
+            for bh in range(2):
+                for g in range(2):
+                    z32 = s1.tile([P, 4, HALF], F32)
+                    for u in range(2):
+                        a = 2 * g + u
+                        eps_bank = psum_tr.tile([P, HALF], F32, tag="tr")
+                        for i in range(4):
+                            nc.tensor.transpose(
+                                eps_bank[:, i * P : (i + 1) * P],
+                                eps_words[:, 4 * bh + i, a * P : (a + 1) * P],
+                                ident[:],
+                            )
+                        sig = s1.tile([P, 2, HALF], F32)
+                        for e in range(2):
+                            row_tile = 2 * a + e
+                            ls_acc = psum_mm.tile([P, HALF], F32, tag="mm")
+                            project(nc, ls_acc, wls_codes, wls_scales, row_tile, x_codes, x_scales, bh)
+                            nc.scalar.activation(
+                                out=sig[:, e, :],
+                                in_=ls_acc[:],
+                                func=ACT.Exp,
+                                bias=bias[:, 8 + row_tile : 9 + row_tile],
+                                scale=0.5,
+                            )
+                        noise = s1.tile([P, HALF, 2], F32)
+                        nc.vector.tensor_tensor(
+                            out=noise[:],
+                            in0=sig[:].rearrange("p e b -> p b e"),
+                            in1=eps_bank[:].bitcast(BF16).rearrange("p (b e) -> p b e", e=2),
+                            op=ALU.mult,
+                        )
+                        for e in range(2):
+                            row_tile = 2 * a + e
+                            mu_acc = psum_mm.tile([P, HALF], F32, tag="mm")
+                            project(nc, mu_acc, wmu_codes, wmu_scales, row_tile, x_codes, x_scales, bh)
+                            nc.vector.scalar_tensor_tensor(
+                                out=z32[:, 2 * u + e, :],
+                                in0=mu_acc[:],
+                                scalar=bias[:, row_tile : row_tile + 1],
+                                in1=noise[:, :, e],
+                                op0=ALU.add,
+                                op1=ALU.add,
+                            )
+                    z_grouped = stage.tile([P, 2, HALF, 4], BF16, tag="grouped", align_bytes=64)
+                    z_view = z32[:].rearrange("p t b -> p b t")
+                    nc.vector.tensor_copy(out=z_grouped[:, 0, :, :], in_=z_view)
+                    nc.scalar.activation(out=z_grouped[:, 1, :, :], in_=z_view, func=ACT.Square)
+                    quantise(nc, z_grouped, z_codes[:, 2 * bh + g], z_scales[:, 2 * bh + g])
+                    z_out = s1.tile([P, 4, HALF], F32)
+                    for i in range(4):
+                        back = psum_tr.tile([P, 4, P], F32, tag="tr")
+                        for t in range(4):
+                            nc.tensor.transpose(back[:, t, :], z32[:, t, i * P : (i + 1) * P], ident[:])
+                        nc.scalar.copy(
+                            out=z_out[:, i, :].rearrange("p (u q e) -> p u q e", u=2, e=2),
+                            in_=back[:].rearrange("p (u e) q -> p u q e", e=2),
+                        )
+                    nc.sync.dma_start(
+                        out=out_0[HALF * bh : HALF * bh + HALF, HALF * g : HALF * g + HALF].rearrange(
+                            "(i r) h -> r i h", r=P
+                        ),
+                        in_=z_out[:],
+                    )
+                for i in range(4):
+                    cols = slice(i * P, (i + 1) * P)
+                    d_acc = psum_mm.tile([P, K], F32, tag="mm")
+                    for g in range(2):
+                        for kind, (c_codes, c_scales) in enumerate(((minv_codes, minv_scales), (inv_codes, inv_scales))):
+                            nc.tensor.matmul_mx(
+                                out=d_acc[:],
+                                lhsT=z_codes[:, 2 * bh + g, kind, cols].bitcast(FP8X4),
+                                lhsT_scale=z_scales[:, 2 * bh + g, kind, cols],
+                                rhs=c_codes[:, g, :].bitcast(FP8X4),
+                                rhs_scale=c_scales[:, g, :],
+                                start=(g == 0 and kind == 0),
+                                stop=(g == 1 and kind == 1),
+                            )
+                    d = s2.tile([P, K], F32)
+                    nc.vector.tensor_tensor(out=d[:], in0=d_acc[:], in1=c2_all[:], op=ALU.add)
+                    d_min = s2.tile([P, 1], F32)
+                    nc.vector.tensor_reduce(out=d_min[:], in_=d[:], axis=mybir.AxisListType.X, op=ALU.min)
+                    weight = s2.tile([P, K], F32)
+                    total = s2.tile([P, 1], F32)
+                    nc.scalar.activation(
+                        out=weight[:], in_=d[:], func=ACT.Exp, bias=d_min[:], scale=-1.0, accum_out=total[:]
+                    )
+                    inv_total = s2.tile([P, 1], F32)
+                    nc.vector.reciprocal(out=inv_total[:], in_=total[:])
+                    att = s2.tile([P, K], F32)
+                    nc.scalar.activation(out=att[:], in_=weight[:], func=ACT.Copy, scale=inv_total[:])
+                    row0 = HALF * bh + i * P
+                    nc.sync.dma_start(out=out_1[row0 : row0 + P, :], in_=att[:])

@@ -1,3 +1,5 @@
+from contextlib import ExitStack
+
 import concourse.mybir as mybir
 from concourse.masks import make_identity
 
@@ -12,6 +14,12 @@ ALU = mybir.AluOpType
 P = 128
 B, H, K = 1024, 1024, 512
 HALF = 512
+PIECE = 256
+UNITS = 8
+
+EARLY = 4
+C2_SLOT = 2
+SLOTS = UNITS + 4
 
 FLOPS = 2 * B * H * H * 2 + 2 * B * K * H * 2
 
@@ -24,7 +32,7 @@ def quantise(nc, grouped, codes, scales):
     )
 
 
-def rows_to_codes(nc, psum_tr, stage, ident, rows, codes, scales):
+def transpose_rows(nc, psum_tr, stage, ident, rows):
     words = rows.bitcast(F32)
     grouped = stage.tile([P, 2, HALF, 4], BF16, tag="grouped", align_bytes=64)
     grouped_words = grouped[:].bitcast(F32)
@@ -32,12 +40,11 @@ def rows_to_codes(nc, psum_tr, stage, ident, rows, codes, scales):
         bank = psum_tr.tile([P, 4, P], F32, tag="tr")
         for j in range(4):
             nc.tensor.transpose(bank[:, j, :], words[:, i, j * P : (j + 1) * P], ident[:])
-        copy_out = nc.scalar.copy if i % 2 == 0 else nc.vector.tensor_copy
-        copy_out(
+        nc.scalar.copy(
             out=grouped_words[:, :, i * P : (i + 1) * P, :],
             in_=bank[:].rearrange("p (g u) r -> p g r u", g=2),
         )
-    quantise(nc, grouped, codes, scales)
+    return grouped
 
 
 def project(nc, bank, w_codes, w_scales, row_tile, x_codes, x_scales, bh):
@@ -59,19 +66,24 @@ def tile_latent_pa_kernel(
     tc, encoder_final_state, W_mu, b_mu, W_ls, b_ls, mu_c, log_sigma_sq_c, eps_z, out_0, out_1
 ):
     nc = tc.nc
-    with tc.tile_pool(name="const", bufs=1) as const, tc.tile_pool(name="raw", bufs=1) as raw, tc.tile_pool(
-        name="codes", bufs=1
-    ) as keep, tc.tile_pool(name="stage", bufs=4) as stage, tc.psum_pool(name="psum_tr", bufs=3) as psum_tr, tc.psum_pool(
-        name="psum_mm", bufs=5
-    ) as psum_mm:
+    with ExitStack() as ctx:
+        ctx.enter_context(tc.manual_schedule())
+        const = ctx.enter_context(tc.tile_pool(name="const", bufs=1))
+        raw = ctx.enter_context(tc.tile_pool(name="raw", bufs=1))
+        keep = ctx.enter_context(tc.tile_pool(name="keep", bufs=1))
+        stage = ctx.enter_context(tc.tile_pool(name="stage", bufs=3))
+        psum_tr = ctx.enter_context(tc.psum_pool(name="psum_tr", bufs=3))
+        psum_mm = ctx.enter_context(tc.psum_pool(name="psum_mm", bufs=5))
+
         ident = const.tile([P, P], F32)
         make_identity(nc, ident[:])
         ones = const.tile([P, P], F32)
         nc.vector.memset(ones[:], 1.0)
         bias_rows = const.tile([P, P], F32)
         nc.vector.memset(bias_rows[:], 0.0)
-        nc.sync.dma_start(out=bias_rows[0:4, :].bitcast(BF16), in_=b_mu.rearrange("(a w) -> a w", a=4))
-        nc.sync.dma_start(out=bias_rows[4:8, :].bitcast(BF16), in_=b_ls.rearrange("(a w) -> a w", a=4))
+        bias = const.tile([P, 16], F32)
+        c2_part = const.tile([P, K], F32)
+        c2_all = const.tile([P, K], F32)
 
         x_nat = raw.tile([P, 8, H], BF16)
         wls_nat = raw.tile([P, 8, H], BF16)
@@ -88,87 +100,40 @@ def tile_latent_pa_kernel(
         inv_scales = keep.tile([P, 2, K], U8, align_bytes=64)
         minv_codes = keep.tile([P, 2, K], U32, align_bytes=64)
         minv_scales = keep.tile([P, 2, K], U8, align_bytes=64)
-        z_codes = keep.tile([P, 4, 2, HALF], U32, align_bytes=64)
-        z_scales = keep.tile([P, 4, 2, HALF], U8, align_bytes=64)
-        c2_all = const.tile([P, K], F32)
-        bias = const.tile([P, 16], F32)
+        z_codes = keep.tile([P, 8, 2, PIECE], U32, align_bytes=64)
+        z_scales = keep.tile([P, 8, 2, PIECE], U8, align_bytes=64)
 
-        with tc.tile_pool(name="cl_raw", bufs=1) as cl_raw, tc.tile_pool(name="cl_tmp", bufs=2) as cl_tmp:
-            ls_nat = cl_raw.tile([P, 4, H], BF16)
-            mu_nat = cl_raw.tile([P, 4, H], BF16)
+        def load_rows(nat, src, half):
+            nc.sync.dma_start(
+                out=nat[:, 4 * half : 4 * half + 4, :],
+                in_=src[HALF * half : HALF * half + HALF, :].rearrange("(t r) h -> r t h", r=P),
+            )
+
+        def load_weight(nat, src, half):
+            nc.sync.dma_start(
+                out=nat[:, 4 * half : 4 * half + 4, :].rearrange("q (a e) h -> q a (e h)", e=2),
+                in_=src[HALF * half : HALF * half + HALF, :].rearrange("(a q e) h -> q a (e h)", q=P, e=2),
+            )
+
+        nc.sync.dma_start(out=bias_rows[0:4, :].bitcast(BF16), in_=b_mu.rearrange("(a w) -> a w", a=4))
+        nc.sync.dma_start(out=bias_rows[4:8, :].bitcast(BF16), in_=b_ls.rearrange("(a w) -> a w", a=4))
+        with tc.tile_pool(name="cl_tmp", bufs=3) as cl_tmp, tc.tile_pool(name="cl_keep", bufs=1) as cl_keep:
+            ls_nat = cl_keep.tile([P, 4, H], BF16)
+            mu_nat = cl_keep.tile([P, 4, H], BF16)
             for ch in range(2):
                 for nat, src in ((ls_nat, log_sigma_sq_c), (mu_nat, mu_c)):
                     nc.sync.dma_start(
                         out=nat[:, 2 * ch : 2 * ch + 2, :],
-                        in_=src[256 * ch : 256 * ch + 256, :].rearrange("(t r) h -> r t h", r=P),
+                        in_=src[PIECE * ch : PIECE * ch + PIECE, :].rearrange("(t r) h -> r t h", r=P),
                     )
-            for half in range(2):
-                nc.sync.dma_start(
-                    out=x_nat[:, 4 * half : 4 * half + 4, :],
-                    in_=encoder_final_state[HALF * half : HALF * half + HALF, :].rearrange("(t r) h -> r t h", r=P),
-                )
-            for half in range(2):
-                for nat, src in ((wls_nat, W_ls), (wmu_nat, W_mu)):
-                    nc.sync.dma_start(
-                        out=nat[:, 4 * half : 4 * half + 4, :].rearrange("q (a e) h -> q a (e h)", e=2),
-                        in_=src[HALF * half : HALF * half + HALF, :].rearrange("(a q e) h -> q a (e h)", q=P, e=2),
-                    )
-            for half in range(2):
-                nc.sync.dma_start(
-                    out=eps_nat[:, 4 * half : 4 * half + 4, :],
-                    in_=eps_z[HALF * half : HALF * half + HALF, :].rearrange("(t r) h -> r t h", r=P),
-                )
-
-            ls_words = ls_nat[:].bitcast(F32)
-            mu_words = mu_nat[:].bitcast(F32)
-            inv_grouped = stage.tile([P, 2, K, 4], BF16, tag="grouped", align_bytes=64)
-            minv_grouped = stage.tile([P, 2, K, 4], BF16, tag="grouped", align_bytes=64)
-            prod = cl_raw.tile([P, 2, 4, K], F32)
-            for g in range(2):
-                for ch in range(2):
-                    cols = slice(256 * ch, 256 * ch + 256)
-                    ls_bank = psum_tr.tile([P, 2, 256], F32, tag="tr")
-                    mu_bank = psum_tr.tile([P, 2, 256], F32, tag="tr")
-                    for bank, words in ((ls_bank, ls_words), (mu_bank, mu_words)):
-                        for u in range(2):
-                            for j in range(2):
-                                nc.tensor.transpose(
-                                    bank[:, u, j * P : (j + 1) * P],
-                                    words[:, 2 * ch + j, (2 * g + u) * P : (2 * g + u + 1) * P],
-                                    ident[:],
-                                )
-                    ls_view = ls_bank[:].bitcast(BF16).rearrange("p u (c e) -> p c u e", e=2)
-                    mu_view = mu_bank[:].bitcast(BF16).rearrange("p u (c e) -> p c u e", e=2)
-                    inv32 = cl_tmp.tile([P, 256, 2, 2], F32)
-                    nc.scalar.activation(out=inv32[:], in_=ls_view, func=ACT.Exp, scale=-1.0)
-                    nc.scalar.activation(
-                        out=inv_grouped[:, g, cols, :].rearrange("p c (u e) -> p c u e", e=2),
-                        in_=ls_view,
-                        func=ACT.Exp,
-                        scale=-1.0,
-                    )
-                    minv32 = cl_tmp.tile([P, 256, 2, 2], F32)
-                    nc.vector.tensor_tensor(out=minv32[:], in0=mu_view, in1=inv32[:], op=ALU.mult)
-                    nc.scalar.activation(
-                        out=minv_grouped[:, g, cols, :].rearrange("p c (u e) -> p c u e", e=2),
-                        in_=minv32[:],
-                        func=ACT.Copy,
-                        scale=-2.0,
-                    )
-                    nc.vector.tensor_tensor(
-                        out=prod[:, g, :, cols].rearrange("p (u e) c -> p c u e", e=2),
-                        in0=mu_view,
-                        in1=minv32[:],
-                        op=ALU.mult,
-                    )
-            quantise(nc, inv_grouped, inv_codes[:], inv_scales[:])
-            quantise(nc, minv_grouped, minv_codes[:], minv_scales[:])
-            c2_bank = psum_mm.tile([P, K], F32, tag="mm")
-            for n in range(8):
-                nc.tensor.matmul(
-                    c2_bank[:], lhsT=ones[:], rhs=prod[:, n // 4, n % 4, :], start=(n == 0), stop=(n == 7)
-                )
-            nc.vector.tensor_copy(out=c2_all[:], in_=c2_bank[:])
+            load_rows(x_nat, encoder_final_state, 0)
+            load_weight(wls_nat, W_ls, 0)
+            load_weight(wmu_nat, W_mu, 0)
+            load_rows(eps_nat, eps_z, 0)
+            load_weight(wls_nat, W_ls, 1)
+            load_weight(wmu_nat, W_mu, 1)
+            load_rows(x_nat, encoder_final_state, 1)
+            load_rows(eps_nat, eps_z, 1)
 
             bias_bank = psum_tr.tile([P, P], F32, tag="tr")
             nc.tensor.transpose(bias_bank[:], bias_rows[:], ident[:])
@@ -177,109 +142,253 @@ def tile_latent_pa_kernel(
                 out=bias[:, 8:16], in0=bias_bank[:, 4:8].bitcast(BF16), scalar1=0.5, scalar2=None, op0=ALU.mult
             )
 
-        for half in range(2):
-            rows_to_codes(
-                nc, psum_tr, stage, ident, x_nat[:, 4 * half : 4 * half + 4, :], x_codes[:, half], x_scales[:, half]
-            )
-        for half in range(2):
-            rows_to_codes(
-                nc, psum_tr, stage, ident, wls_nat[:, 4 * half : 4 * half + 4, :], wls_codes[:, half], wls_scales[:, half]
-            )
-            rows_to_codes(
-                nc, psum_tr, stage, ident, wmu_nat[:, 4 * half : 4 * half + 4, :], wmu_codes[:, half], wmu_scales[:, half]
-            )
-
-        eps_words = eps_nat[:].bitcast(F32)
-        with tc.tile_pool(name="s1", bufs=2) as s1, tc.tile_pool(name="s2", bufs=2) as s2:
-            for bh in range(2):
-                for g in range(2):
-                    z32 = s1.tile([P, 4, HALF], F32)
+            ls_words = ls_nat[:].bitcast(F32)
+            mu_words = mu_nat[:].bitcast(F32)
+            inv_grouped = cl_keep.tile([P, 2, K, 4], BF16, align_bytes=64)
+            minv_grouped = cl_keep.tile([P, 2, K, 4], BF16, align_bytes=64)
+            prod = cl_keep.tile([P, 2, 4, K], F32)
+            items = [(ch, g) for ch in range(2) for g in range(2)]
+            mu_views = []
+            inv32s = []
+            for ch, g in items:
+                ls_bank = psum_mm.tile([P, 2, PIECE], F32, tag="mm")
+                mu_bank = psum_mm.tile([P, 2, PIECE], F32, tag="mm")
+                for bank, words in ((ls_bank, ls_words), (mu_bank, mu_words)):
                     for u in range(2):
-                        a = 2 * g + u
-                        eps_bank = psum_tr.tile([P, HALF], F32, tag="tr")
-                        for i in range(4):
+                        for j in range(2):
                             nc.tensor.transpose(
-                                eps_bank[:, i * P : (i + 1) * P],
-                                eps_words[:, 4 * bh + i, a * P : (a + 1) * P],
+                                bank[:, u, j * P : (j + 1) * P],
+                                words[:, 2 * ch + j, (2 * g + u) * P : (2 * g + u + 1) * P],
                                 ident[:],
                             )
-                        sig = s1.tile([P, 2, HALF], F32)
-                        for e in range(2):
-                            row_tile = 2 * a + e
-                            ls_acc = psum_mm.tile([P, HALF], F32, tag="mm")
-                            project(nc, ls_acc, wls_codes, wls_scales, row_tile, x_codes, x_scales, bh)
-                            nc.scalar.activation(
-                                out=sig[:, e, :],
-                                in_=ls_acc[:],
-                                func=ACT.Exp,
-                                bias=bias[:, 8 + row_tile : 9 + row_tile],
-                                scale=0.5,
-                            )
-                        noise = s1.tile([P, HALF, 2], F32)
-                        nc.vector.tensor_tensor(
-                            out=noise[:],
-                            in0=sig[:].rearrange("p e b -> p b e"),
-                            in1=eps_bank[:].bitcast(BF16).rearrange("p (b e) -> p b e", e=2),
-                            op=ALU.mult,
+                mu_views.append(mu_bank[:].bitcast(BF16).rearrange("p u (c e) -> p c u e", e=2))
+                inv32 = cl_tmp.tile([P, PIECE, 2, 2], F32)
+                nc.scalar.activation(
+                    out=inv32[:],
+                    in_=ls_bank[:].bitcast(BF16).rearrange("p u (c e) -> p c u e", e=2),
+                    func=ACT.Exp,
+                    scale=-1.0,
+                )
+                inv32s.append(inv32)
+            for n, (ch, g) in enumerate(items):
+                cols = slice(PIECE * ch, PIECE * ch + PIECE)
+                nc.gpsimd.tensor_scalar(
+                    out=inv_grouped[:, g, cols, :].rearrange("p c (u e) -> p c u e", e=2),
+                    in0=inv32s[n][:],
+                    scalar1=1.0,
+                    scalar2=0.0,
+                    op0=ALU.mult,
+                    op1=ALU.add,
+                )
+                minv32 = cl_tmp.tile([P, PIECE, 2, 2], F32)
+                nc.vector.tensor_tensor(out=minv32[:], in0=mu_views[n], in1=inv32s[n][:], op=ALU.mult)
+                nc.gpsimd.tensor_scalar(
+                    out=minv_grouped[:, g, cols, :].rearrange("p c (u e) -> p c u e", e=2),
+                    in0=minv32[:],
+                    scalar1=-2.0,
+                    scalar2=0.0,
+                    op0=ALU.mult,
+                    op1=ALU.add,
+                )
+                nc.vector.tensor_tensor(
+                    out=prod[:, g, :, cols].rearrange("p (u e) c -> p c u e", e=2),
+                    in0=mu_views[n],
+                    in1=minv32[:],
+                    op=ALU.mult,
+                )
+            nc.gpsimd.tensor_tensor(out=prod[:, :, 0, :], in0=prod[:, :, 0, :], in1=prod[:, :, 1, :], op=ALU.add)
+            nc.gpsimd.tensor_tensor(out=prod[:, :, 2, :], in0=prod[:, :, 2, :], in1=prod[:, :, 3, :], op=ALU.add)
+            nc.gpsimd.tensor_tensor(out=prod[:, :, 0, :], in0=prod[:, :, 0, :], in1=prod[:, :, 2, :], op=ALU.add)
+            nc.gpsimd.tensor_tensor(out=c2_part[:], in0=prod[:, 0, 0, :], in1=prod[:, 1, 0, :], op=ALU.add)
+
+            operands = [
+                (x_nat, x_codes, x_scales, 0),
+                (wls_nat, wls_codes, wls_scales, 0),
+                (wmu_nat, wmu_codes, wmu_scales, 0),
+                (wls_nat, wls_codes, wls_scales, 1),
+                (wmu_nat, wmu_codes, wmu_scales, 1),
+                (x_nat, x_codes, x_scales, 1),
+            ]
+            grouped_of = {}
+
+            def operand_transposes(n):
+                nat, codes, scales, half = operands[n]
+                grouped_of[n] = transpose_rows(nc, psum_tr, stage, ident, nat[:, 4 * half : 4 * half + 4, :])
+
+            def operand_quantise(n):
+                nat, codes, scales, half = operands[n]
+                quantise(nc, grouped_of[n], codes[:, half], scales[:, half])
+
+            for n in range(EARLY):
+                operand_transposes(n)
+                if n > 0:
+                    operand_quantise(n - 1)
+            quantise(nc, inv_grouped, inv_codes[:], inv_scales[:])
+            quantise(nc, minv_grouped, minv_codes[:], minv_scales[:])
+
+        s1 = ctx.enter_context(tc.tile_pool(name="s1", bufs=2, reuse_waits="tile"))
+        s3 = ctx.enter_context(tc.tile_pool(name="s3", bufs=3, reuse_waits="tile"))
+        eps_words = eps_nat[:].bitcast(F32)
+        eps_banks = {}
+        z32s = {}
+        z_groupeds = {}
+        d_accs = {}
+
+        def eps_transposes(s):
+            bh, a = divmod(s, 4)
+            eps_bank = psum_tr.tile([P, HALF], F32, tag="tr")
+            for i in range(4):
+                nc.tensor.transpose(
+                    eps_bank[:, i * P : (i + 1) * P], eps_words[:, 4 * bh + i, a * P : (a + 1) * P], ident[:]
+                )
+            eps_banks[s] = eps_bank
+
+        def unit_sigma(s):
+            bh, a = divmod(s, 4)
+            sig = s1.tile([P, 2, HALF], F32, tag="sig")
+            for e in range(2):
+                row_tile = 2 * a + e
+                ls_acc = psum_mm.tile([P, HALF], F32, tag="mm")
+                project(nc, ls_acc, wls_codes, wls_scales, row_tile, x_codes, x_scales, bh)
+                nc.scalar.activation(
+                    out=sig[:, e, :],
+                    in_=ls_acc[:],
+                    func=ACT.Exp,
+                    bias=bias[:, 8 + row_tile : 9 + row_tile],
+                    scale=0.5,
+                )
+            return sig
+
+        def unit_z(s, sig):
+            bh, a = divmod(s, 4)
+            u = a % 2
+            if u == 0:
+                z32 = s1.tile([P, 4, HALF], F32, tag="z32")
+                z32s[s // 2] = z32
+            noise = s1.tile([P, HALF, 2], F32, tag="noise")
+            nc.vector.tensor_tensor(
+                out=noise[:],
+                in0=sig[:].rearrange("p e b -> p b e"),
+                in1=eps_banks[s][:].bitcast(BF16).rearrange("p (b e) -> p b e", e=2),
+                op=ALU.mult,
+            )
+            for e in range(2):
+                row_tile = 2 * a + e
+                mu_acc = psum_mm.tile([P, HALF], F32, tag="mm")
+                project(nc, mu_acc, wmu_codes, wmu_scales, row_tile, x_codes, x_scales, bh)
+                nc.vector.scalar_tensor_tensor(
+                    out=z32s[s // 2][:, 2 * u + e, :],
+                    in0=mu_acc[:],
+                    scalar=bias[:, row_tile : row_tile + 1],
+                    in1=noise[:, :, e],
+                    op0=ALU.add,
+                    op1=ALU.add,
+                )
+
+        def regroup(j, p):
+            z_view = z32s[j][:, :, p * PIECE : (p + 1) * PIECE].rearrange("p t b -> p b t")
+            z_grouped = s3.tile([P, 2, PIECE, 4], BF16, tag="z_grouped", align_bytes=64)
+            nc.gpsimd.tensor_scalar(
+                out=z_grouped[:, 0, :, :], in0=z_view, scalar1=1.0, scalar2=0.0, op0=ALU.mult, op1=ALU.add
+            )
+            nc.scalar.activation(out=z_grouped[:, 1, :, :], in_=z_view, func=ACT.Square)
+            z_groupeds[(j, p)] = z_grouped
+
+        def store_z(j, p):
+            bh, g = divmod(j, 2)
+            z_out = s3.tile([P, 2, HALF], F32, tag="z_out")
+            for i in range(2):
+                first = (2 * p + i) * P
+                back = psum_tr.tile([P, 4, P], F32, tag="tr")
+                for t in range(4):
+                    nc.tensor.transpose(back[:, t, :], z32s[j][:, t, first : first + P], ident[:])
+                nc.scalar.copy(
+                    out=z_out[:, i, :].rearrange("p (u q e) -> p u q e", u=2, e=2),
+                    in_=back[:].rearrange("p (u e) q -> p u q e", e=2),
+                )
+            row0 = HALF * bh + PIECE * p
+            nc.sync.dma_start(
+                out=out_0[row0 : row0 + PIECE, HALF * g : HALF * g + HALF].rearrange("(i r) h -> r i h", r=P),
+                in_=z_out[:],
+            )
+
+        def distances(bh, p):
+            for i in range(2):
+                cols = slice(i * P, (i + 1) * P)
+                d_acc = psum_mm.tile([P, K], F32, tag="mm")
+                for g in range(2):
+                    piece = 2 * (2 * bh + g) + p
+                    for kind, (c_codes, c_scales) in enumerate(((minv_codes, minv_scales), (inv_codes, inv_scales))):
+                        nc.tensor.matmul_mx(
+                            out=d_acc[:],
+                            lhsT=z_codes[:, piece, kind, cols].bitcast(FP8X4),
+                            lhsT_scale=z_scales[:, piece, kind, cols],
+                            rhs=c_codes[:, g, :].bitcast(FP8X4),
+                            rhs_scale=c_scales[:, g, :],
+                            start=(g == 0 and kind == 0),
+                            stop=(g == 1 and kind == 1),
                         )
-                        for e in range(2):
-                            row_tile = 2 * a + e
-                            mu_acc = psum_mm.tile([P, HALF], F32, tag="mm")
-                            project(nc, mu_acc, wmu_codes, wmu_scales, row_tile, x_codes, x_scales, bh)
-                            nc.vector.scalar_tensor_tensor(
-                                out=z32[:, 2 * u + e, :],
-                                in0=mu_acc[:],
-                                scalar=bias[:, row_tile : row_tile + 1],
-                                in1=noise[:, :, e],
-                                op0=ALU.add,
-                                op1=ALU.add,
-                            )
-                    z_grouped = stage.tile([P, 2, HALF, 4], BF16, tag="grouped", align_bytes=64)
-                    z_view = z32[:].rearrange("p t b -> p b t")
-                    nc.vector.tensor_copy(out=z_grouped[:, 0, :, :], in_=z_view)
-                    nc.scalar.activation(out=z_grouped[:, 1, :, :], in_=z_view, func=ACT.Square)
-                    quantise(nc, z_grouped, z_codes[:, 2 * bh + g], z_scales[:, 2 * bh + g])
-                    z_out = s1.tile([P, 4, HALF], F32)
-                    for i in range(4):
-                        back = psum_tr.tile([P, 4, P], F32, tag="tr")
-                        for t in range(4):
-                            nc.tensor.transpose(back[:, t, :], z32[:, t, i * P : (i + 1) * P], ident[:])
-                        nc.scalar.copy(
-                            out=z_out[:, i, :].rearrange("p (u q e) -> p u q e", u=2, e=2),
-                            in_=back[:].rearrange("p (u e) q -> p u q e", e=2),
-                        )
-                    nc.sync.dma_start(
-                        out=out_0[HALF * bh : HALF * bh + HALF, HALF * g : HALF * g + HALF].rearrange(
-                            "(i r) h -> r i h", r=P
-                        ),
-                        in_=z_out[:],
-                    )
-                for i in range(4):
-                    cols = slice(i * P, (i + 1) * P)
-                    d_acc = psum_mm.tile([P, K], F32, tag="mm")
-                    for g in range(2):
-                        for kind, (c_codes, c_scales) in enumerate(((minv_codes, minv_scales), (inv_codes, inv_scales))):
-                            nc.tensor.matmul_mx(
-                                out=d_acc[:],
-                                lhsT=z_codes[:, 2 * bh + g, kind, cols].bitcast(FP8X4),
-                                lhsT_scale=z_scales[:, 2 * bh + g, kind, cols],
-                                rhs=c_codes[:, g, :].bitcast(FP8X4),
-                                rhs_scale=c_scales[:, g, :],
-                                start=(g == 0 and kind == 0),
-                                stop=(g == 1 and kind == 1),
-                            )
-                    d = s2.tile([P, K], F32)
-                    nc.vector.tensor_tensor(out=d[:], in0=d_acc[:], in1=c2_all[:], op=ALU.add)
-                    d_min = s2.tile([P, 1], F32)
-                    nc.vector.tensor_reduce(out=d_min[:], in_=d[:], axis=mybir.AxisListType.X, op=ALU.min)
-                    weight = s2.tile([P, K], F32)
-                    total = s2.tile([P, 1], F32)
-                    nc.scalar.activation(
-                        out=weight[:], in_=d[:], func=ACT.Exp, bias=d_min[:], scale=-1.0, accum_out=total[:]
-                    )
-                    inv_total = s2.tile([P, 1], F32)
-                    nc.vector.reciprocal(out=inv_total[:], in_=total[:])
-                    att = s2.tile([P, K], F32)
-                    nc.scalar.activation(out=att[:], in_=weight[:], func=ACT.Copy, scale=inv_total[:])
-                    row0 = HALF * bh + i * P
-                    nc.sync.dma_start(out=out_1[row0 : row0 + P, :], in_=att[:])
+                d_accs[(bh, p, i)] = d_acc
+
+        def softmax(bh, p):
+            ds = []
+            d_mins = []
+            weights = []
+            totals = []
+            for i in range(2):
+                d = s1.tile([P, K], F32, tag="d")
+                nc.vector.tensor_tensor(out=d[:], in0=d_accs[(bh, p, i)][:], in1=c2_all[:], op=ALU.add)
+                d_min = s1.tile([P, 1], F32, tag="d_min")
+                nc.vector.tensor_reduce(out=d_min[:], in_=d[:], axis=mybir.AxisListType.X, op=ALU.min)
+                ds.append(d)
+                d_mins.append(d_min)
+            for i in range(2):
+                weight = s1.tile([P, K], F32, tag="weight")
+                total = s1.tile([P, 1], F32, tag="total")
+                nc.scalar.activation(
+                    out=weight[:], in_=ds[i][:], func=ACT.Exp, bias=d_mins[i][:], scale=-1.0, accum_out=total[:]
+                )
+                weights.append(weight)
+                totals.append(total)
+            for i in range(2):
+                inv_total = s1.tile([P, 1], F32, tag="inv_total")
+                nc.vector.reciprocal(out=inv_total[:], in_=totals[i][:])
+                att = s1.tile([P, K], F32, tag="att")
+                nc.gpsimd.tensor_scalar(
+                    out=att[:], in0=weights[i][:], scalar1=inv_total[:], scalar2=0.0, op0=ALU.mult, op1=ALU.add
+                )
+                row0 = HALF * bh + PIECE * p + i * P
+                nc.sync.dma_start(out=out_1[row0 : row0 + P, :], in_=att[:])
+
+        def pair_at(s):
+            bh, p = divmod(s - 5, 4)
+            return (bh, p) if s >= 5 and bh < 2 and p < 2 else None
+
+        eps_transposes(0)
+        for s in range(SLOTS):
+            if s < UNITS:
+                sig = unit_sigma(s)
+            if pair_at(s - 1) is not None:
+                softmax(*pair_at(s - 1))
+            if EARLY - 1 + s < len(operands):
+                operand_quantise(EARLY - 1 + s)
+            if s == C2_SLOT + 1:
+                nc.vector.tensor_copy(out=c2_all[:], in_=c2_bank[:])
+            if 3 <= s < 3 + UNITS:
+                j, p = divmod(s - 3, 2)
+                quantise(nc, z_groupeds[(j, p)], z_codes[:, 2 * j + p], z_scales[:, 2 * j + p])
+            if s < UNITS:
+                unit_z(s, sig)
+            if pair_at(s) is not None:
+                distances(*pair_at(s))
+            if 2 <= s < 2 + UNITS:
+                j, p = divmod(s - 2, 2)
+                regroup(j, p)
+                store_z(j, p)
+            if EARLY + s < len(operands):
+                operand_transposes(EARLY + s)
+            if s == C2_SLOT:
+                c2_bank = psum_tr.tile([P, K], F32, tag="tr")
+                nc.tensor.matmul(c2_bank[:], lhsT=ones[:], rhs=c2_part[:], start=True, stop=True)
+            if s + 1 < UNITS:
+                eps_transposes(s + 1)

@@ -72,8 +72,8 @@ def tile_latent_pa_kernel(
         raw = ctx.enter_context(tc.tile_pool(name="raw", bufs=1))
         keep = ctx.enter_context(tc.tile_pool(name="keep", bufs=1))
         stage = ctx.enter_context(tc.tile_pool(name="stage", bufs=3))
-        psum_tr = ctx.enter_context(tc.psum_pool(name="psum_tr", bufs=3))
-        psum_mm = ctx.enter_context(tc.psum_pool(name="psum_mm", bufs=5))
+        psum_tr = ctx.enter_context(tc.psum_pool(name="psum_tr", bufs=4))
+        psum_mm = ctx.enter_context(tc.psum_pool(name="psum_mm", bufs=4))
 
         ident = const.tile([P, P], F32)
         make_identity(nc, ident[:])
@@ -170,7 +170,10 @@ def tile_latent_pa_kernel(
                     scale=-1.0,
                 )
                 inv32s.append(inv32)
-            for n, (ch, g) in enumerate(items):
+            minv32s = []
+
+            def scaled_means(n):
+                ch, g = items[n]
                 cols = slice(PIECE * ch, PIECE * ch + PIECE)
                 nc.gpsimd.tensor_scalar(
                     out=inv_grouped[:, g, cols, :].rearrange("p c (u e) -> p c u e", e=2),
@@ -190,12 +193,23 @@ def tile_latent_pa_kernel(
                     op0=ALU.mult,
                     op1=ALU.add,
                 )
+                minv32s.append(minv32)
+
+            def c2_terms(n):
+                ch, g = items[n]
+                cols = slice(PIECE * ch, PIECE * ch + PIECE)
                 nc.vector.tensor_tensor(
                     out=prod[:, g, :, cols].rearrange("p (u e) c -> p c u e", e=2),
                     in0=mu_views[n],
-                    in1=minv32[:],
+                    in1=minv32s[n][:],
                     op=ALU.mult,
                 )
+
+            scaled_means(0)
+            for n in range(1, len(items)):
+                scaled_means(n)
+                c2_terms(n - 1)
+            c2_terms(len(items) - 1)
             nc.gpsimd.tensor_tensor(out=prod[:, :, 0, :], in0=prod[:, :, 0, :], in1=prod[:, :, 1, :], op=ALU.add)
             nc.gpsimd.tensor_tensor(out=prod[:, :, 2, :], in0=prod[:, :, 2, :], in1=prod[:, :, 3, :], op=ALU.add)
             nc.gpsimd.tensor_tensor(out=prod[:, :, 0, :], in0=prod[:, :, 0, :], in1=prod[:, :, 2, :], op=ALU.add)
@@ -233,6 +247,8 @@ def tile_latent_pa_kernel(
         z32s = {}
         z_groupeds = {}
         d_accs = {}
+        z_outs = {}
+        soft = {}
 
         def eps_transposes(s):
             bh, a = divmod(s, 4)
@@ -259,12 +275,7 @@ def tile_latent_pa_kernel(
                 )
             return sig
 
-        def unit_z(s, sig):
-            bh, a = divmod(s, 4)
-            u = a % 2
-            if u == 0:
-                z32 = s1.tile([P, 4, HALF], F32, tag="z32")
-                z32s[s // 2] = z32
+        def unit_noise(s, sig):
             noise = s1.tile([P, HALF, 2], F32, tag="noise")
             nc.vector.tensor_tensor(
                 out=noise[:],
@@ -272,6 +283,14 @@ def tile_latent_pa_kernel(
                 in1=eps_banks[s][:].bitcast(BF16).rearrange("p (b e) -> p b e", e=2),
                 op=ALU.mult,
             )
+            return noise
+
+        def unit_z(s, noise):
+            bh, a = divmod(s, 4)
+            u = a % 2
+            if u == 0:
+                z32 = s1.tile([P, 4, HALF], F32, tag="z32")
+                z32s[s // 2] = z32
             for e in range(2):
                 row_tile = 2 * a + e
                 mu_acc = psum_mm.tile([P, HALF], F32, tag="mm")
@@ -294,22 +313,26 @@ def tile_latent_pa_kernel(
             nc.scalar.activation(out=z_grouped[:, 1, :, :], in_=z_view, func=ACT.Square)
             z_groupeds[(j, p)] = z_grouped
 
+        def z_back(j, p, i):
+            if i == 0:
+                z_out = s3.tile([P, 2, HALF], F32, tag="z_out")
+                z_outs[(j, p)] = z_out
+            first = (2 * p + i) * P
+            back = psum_tr.tile([P, 4, P], F32, tag="tr")
+            for t in range(4):
+                nc.tensor.transpose(back[:, t, :], z32s[j][:, t, first : first + P], ident[:])
+            copy_out = nc.scalar.copy if i == 0 else nc.vector.tensor_copy
+            copy_out(
+                out=z_outs[(j, p)][:, i, :].rearrange("p (u q e) -> p u q e", u=2, e=2),
+                in_=back[:].rearrange("p (u e) q -> p u q e", e=2),
+            )
+
         def store_z(j, p):
             bh, g = divmod(j, 2)
-            z_out = s3.tile([P, 2, HALF], F32, tag="z_out")
-            for i in range(2):
-                first = (2 * p + i) * P
-                back = psum_tr.tile([P, 4, P], F32, tag="tr")
-                for t in range(4):
-                    nc.tensor.transpose(back[:, t, :], z32s[j][:, t, first : first + P], ident[:])
-                nc.scalar.copy(
-                    out=z_out[:, i, :].rearrange("p (u q e) -> p u q e", u=2, e=2),
-                    in_=back[:].rearrange("p (u e) q -> p u q e", e=2),
-                )
             row0 = HALF * bh + PIECE * p
             nc.sync.dma_start(
                 out=out_0[row0 : row0 + PIECE, HALF * g : HALF * g + HALF].rearrange("(i r) h -> r i h", r=P),
-                in_=z_out[:],
+                in_=z_outs[(j, p)][:],
             )
 
         def distances(bh, p):
@@ -330,18 +353,23 @@ def tile_latent_pa_kernel(
                         )
                 d_accs[(bh, p, i)] = d_acc
 
-        def softmax(bh, p):
+        def softmax_min(bh, p):
             ds = []
-            d_mins = []
-            weights = []
-            totals = []
             for i in range(2):
                 d = s1.tile([P, K], F32, tag="d")
                 nc.vector.tensor_tensor(out=d[:], in0=d_accs[(bh, p, i)][:], in1=c2_all[:], op=ALU.add)
-                d_min = s1.tile([P, 1], F32, tag="d_min")
-                nc.vector.tensor_reduce(out=d_min[:], in_=d[:], axis=mybir.AxisListType.X, op=ALU.min)
                 ds.append(d)
+            d_mins = []
+            for i in range(2):
+                d_min = s1.tile([P, 1], F32, tag="d_min")
+                nc.vector.tensor_reduce(out=d_min[:], in_=ds[i][:], axis=mybir.AxisListType.X, op=ALU.min)
                 d_mins.append(d_min)
+            soft[(bh, p)] = (ds, d_mins)
+
+        def softmax_exp(bh, p):
+            ds, d_mins = soft[(bh, p)]
+            weights = []
+            totals = []
             for i in range(2):
                 weight = s1.tile([P, K], F32, tag="weight")
                 total = s1.tile([P, 1], F32, tag="total")
@@ -350,6 +378,10 @@ def tile_latent_pa_kernel(
                 )
                 weights.append(weight)
                 totals.append(total)
+            soft[(bh, p)] = (weights, totals)
+
+        def softmax_norm(bh, p):
+            weights, totals = soft[(bh, p)]
             for i in range(2):
                 inv_total = s1.tile([P, 1], F32, tag="inv_total")
                 nc.vector.reciprocal(out=inv_total[:], in_=totals[i][:])
@@ -366,10 +398,15 @@ def tile_latent_pa_kernel(
 
         eps_transposes(0)
         for s in range(SLOTS):
+            last_pair = pair_at(s - 1)
+            piece = divmod(s - 2, 2) if 2 <= s < 2 + UNITS else None
             if s < UNITS:
                 sig = unit_sigma(s)
-            if pair_at(s - 1) is not None:
-                softmax(*pair_at(s - 1))
+            if last_pair is not None:
+                softmax_min(*last_pair)
+                softmax_exp(*last_pair)
+            if s < UNITS:
+                noise = unit_noise(s, sig)
             if EARLY - 1 + s < len(operands):
                 operand_quantise(EARLY - 1 + s)
             if s == C2_SLOT + 1:
@@ -377,14 +414,18 @@ def tile_latent_pa_kernel(
             if 3 <= s < 3 + UNITS:
                 j, p = divmod(s - 3, 2)
                 quantise(nc, z_groupeds[(j, p)], z_codes[:, 2 * j + p], z_scales[:, 2 * j + p])
+            if piece is not None:
+                z_back(piece[0], piece[1], 0)
             if s < UNITS:
-                unit_z(s, sig)
+                unit_z(s, noise)
+            if last_pair is not None:
+                softmax_norm(*last_pair)
             if pair_at(s) is not None:
                 distances(*pair_at(s))
-            if 2 <= s < 2 + UNITS:
-                j, p = divmod(s - 2, 2)
-                regroup(j, p)
-                store_z(j, p)
+            if piece is not None:
+                regroup(*piece)
+                z_back(piece[0], piece[1], 1)
+                store_z(*piece)
             if EARLY + s < len(operands):
                 operand_transposes(EARLY + s)
             if s == C2_SLOT:

@@ -16,10 +16,11 @@ B, H, K = 1024, 1024, 512
 HALF = 512
 PIECE = 256
 UNITS = 8
-
 EARLY = 4
 C2_SLOT = 2
-SLOTS = UNITS + 4
+REGROUP_LAG = 2
+QUANTISE_LAG = REGROUP_LAG + 1
+SLOTS = UNITS + QUANTISE_LAG + 1
 
 FLOPS = 2 * B * H * H * 2 + 2 * B * K * H * 2
 
@@ -129,8 +130,8 @@ def tile_latent_pa_kernel(
             load_rows(x_nat, encoder_final_state, 0)
             load_weight(wls_nat, W_ls, 0)
             load_weight(wmu_nat, W_mu, 0)
-            load_rows(eps_nat, eps_z, 0)
             load_weight(wls_nat, W_ls, 1)
+            load_rows(eps_nat, eps_z, 0)
             load_weight(wmu_nat, W_mu, 1)
             load_rows(x_nat, encoder_final_state, 1)
             load_rows(eps_nat, eps_z, 1)
@@ -151,7 +152,7 @@ def tile_latent_pa_kernel(
             mu_views = []
             inv32s = []
             for ch, g in items:
-                ls_bank = psum_mm.tile([P, 2, PIECE], F32, tag="mm")
+                ls_bank = psum_tr.tile([P, 2, PIECE], F32, tag="tr")
                 mu_bank = psum_mm.tile([P, 2, PIECE], F32, tag="mm")
                 for bank, words in ((ls_bank, ls_words), (mu_bank, mu_words)):
                     for u in range(2):
@@ -240,14 +241,15 @@ def tile_latent_pa_kernel(
             quantise(nc, inv_grouped, inv_codes[:], inv_scales[:])
             quantise(nc, minv_grouped, minv_codes[:], minv_scales[:])
 
-        s1 = ctx.enter_context(tc.tile_pool(name="s1", bufs=2, reuse_waits="tile"))
-        s3 = ctx.enter_context(tc.tile_pool(name="s3", bufs=3, reuse_waits="tile"))
+        two = ctx.enter_context(tc.tile_pool(name="two", bufs=2, reuse_waits="tile"))
+        three = ctx.enter_context(tc.tile_pool(name="three", bufs=3, reuse_waits="tile"))
         eps_words = eps_nat[:].bitcast(F32)
         eps_banks = {}
+        sigs = {}
         z32s = {}
         z_groupeds = {}
-        d_accs = {}
         z_outs = {}
+        d_accs = {}
         soft = {}
 
         def eps_transposes(s):
@@ -261,7 +263,7 @@ def tile_latent_pa_kernel(
 
         def unit_sigma(s):
             bh, a = divmod(s, 4)
-            sig = s1.tile([P, 2, HALF], F32, tag="sig")
+            sig = three.tile([P, 2, HALF], F32, tag="sig")
             for e in range(2):
                 row_tile = 2 * a + e
                 ls_acc = psum_mm.tile([P, HALF], F32, tag="mm")
@@ -273,13 +275,13 @@ def tile_latent_pa_kernel(
                     bias=bias[:, 8 + row_tile : 9 + row_tile],
                     scale=0.5,
                 )
-            return sig
+            sigs[s] = sig
 
-        def unit_noise(s, sig):
-            noise = s1.tile([P, HALF, 2], F32, tag="noise")
+        def unit_noise(s):
+            noise = two.tile([P, HALF, 2], F32, tag="noise")
             nc.vector.tensor_tensor(
                 out=noise[:],
-                in0=sig[:].rearrange("p e b -> p b e"),
+                in0=sigs[s][:].rearrange("p e b -> p b e"),
                 in1=eps_banks[s][:].bitcast(BF16).rearrange("p (b e) -> p b e", e=2),
                 op=ALU.mult,
             )
@@ -289,7 +291,7 @@ def tile_latent_pa_kernel(
             bh, a = divmod(s, 4)
             u = a % 2
             if u == 0:
-                z32 = s1.tile([P, 4, HALF], F32, tag="z32")
+                z32 = three.tile([P, 4, HALF], F32, tag="z32")
                 z32s[s // 2] = z32
             for e in range(2):
                 row_tile = 2 * a + e
@@ -306,33 +308,32 @@ def tile_latent_pa_kernel(
 
         def regroup(j, p):
             z_view = z32s[j][:, :, p * PIECE : (p + 1) * PIECE].rearrange("p t b -> p b t")
-            z_grouped = s3.tile([P, 2, PIECE, 4], BF16, tag="z_grouped", align_bytes=64)
+            z_grouped = three.tile([P, 2, PIECE, 4], BF16, tag="z_grouped", align_bytes=64)
             nc.gpsimd.tensor_scalar(
                 out=z_grouped[:, 0, :, :], in0=z_view, scalar1=1.0, scalar2=0.0, op0=ALU.mult, op1=ALU.add
             )
             nc.scalar.activation(out=z_grouped[:, 1, :, :], in_=z_view, func=ACT.Square)
             z_groupeds[(j, p)] = z_grouped
 
-        def z_back(j, p, i):
-            if i == 0:
-                z_out = s3.tile([P, 2, HALF], F32, tag="z_out")
-                z_outs[(j, p)] = z_out
-            first = (2 * p + i) * P
-            back = psum_tr.tile([P, 4, P], F32, tag="tr")
-            for t in range(4):
-                nc.tensor.transpose(back[:, t, :], z32s[j][:, t, first : first + P], ident[:])
-            copy_out = nc.scalar.copy if i == 0 else nc.vector.tensor_copy
-            copy_out(
-                out=z_outs[(j, p)][:, i, :].rearrange("p (u q e) -> p u q e", u=2, e=2),
-                in_=back[:].rearrange("p (u e) q -> p u q e", e=2),
-            )
+        def quantise_z(j, p):
+            quantise(nc, z_groupeds[(j, p)], z_codes[:, 2 * j + p], z_scales[:, 2 * j + p])
 
         def store_z(j, p):
             bh, g = divmod(j, 2)
+            z_out = three.tile([P, 2, HALF], F32, tag="z_out")
+            for i in range(2):
+                first = (2 * p + i) * P
+                back = psum_tr.tile([P, 4, P], F32, tag="tr")
+                for t in range(4):
+                    nc.tensor.transpose(back[:, t, :], z32s[j][:, t, first : first + P], ident[:])
+                nc.scalar.copy(
+                    out=z_out[:, i, :].rearrange("p (u q e) -> p u q e", u=2, e=2),
+                    in_=back[:].rearrange("p (u e) q -> p u q e", e=2),
+                )
             row0 = HALF * bh + PIECE * p
             nc.sync.dma_start(
                 out=out_0[row0 : row0 + PIECE, HALF * g : HALF * g + HALF].rearrange("(i r) h -> r i h", r=P),
-                in_=z_outs[(j, p)][:],
+                in_=z_out[:],
             )
 
         def distances(bh, p):
@@ -356,12 +357,12 @@ def tile_latent_pa_kernel(
         def softmax_min(bh, p):
             ds = []
             for i in range(2):
-                d = s1.tile([P, K], F32, tag="d")
+                d = two.tile([P, K], F32, tag="d")
                 nc.vector.tensor_tensor(out=d[:], in0=d_accs[(bh, p, i)][:], in1=c2_all[:], op=ALU.add)
                 ds.append(d)
             d_mins = []
             for i in range(2):
-                d_min = s1.tile([P, 1], F32, tag="d_min")
+                d_min = two.tile([P, 1], F32, tag="d_min")
                 nc.vector.tensor_reduce(out=d_min[:], in_=ds[i][:], axis=mybir.AxisListType.X, op=ALU.min)
                 d_mins.append(d_min)
             soft[(bh, p)] = (ds, d_mins)
@@ -371,8 +372,8 @@ def tile_latent_pa_kernel(
             weights = []
             totals = []
             for i in range(2):
-                weight = s1.tile([P, K], F32, tag="weight")
-                total = s1.tile([P, 1], F32, tag="total")
+                weight = two.tile([P, K], F32, tag="weight")
+                total = two.tile([P, 1], F32, tag="total")
                 nc.scalar.activation(
                     out=weight[:], in_=ds[i][:], func=ACT.Exp, bias=d_mins[i][:], scale=-1.0, accum_out=total[:]
                 )
@@ -383,53 +384,56 @@ def tile_latent_pa_kernel(
         def softmax_norm(bh, p):
             weights, totals = soft[(bh, p)]
             for i in range(2):
-                inv_total = s1.tile([P, 1], F32, tag="inv_total")
+                inv_total = two.tile([P, 1], F32, tag="inv_total")
                 nc.vector.reciprocal(out=inv_total[:], in_=totals[i][:])
-                att = s1.tile([P, K], F32, tag="att")
+                att = two.tile([P, K], F32, tag="att")
                 nc.gpsimd.tensor_scalar(
                     out=att[:], in0=weights[i][:], scalar1=inv_total[:], scalar2=0.0, op0=ALU.mult, op1=ALU.add
                 )
                 row0 = HALF * bh + PIECE * p + i * P
                 nc.sync.dma_start(out=out_1[row0 : row0 + P, :], in_=att[:])
 
-        def pair_at(s):
-            bh, p = divmod(s - 5, 4)
-            return (bh, p) if s >= 5 and bh < 2 and p < 2 else None
+        def piece_at(s):
+            return divmod(s, 2) if 0 <= s < UNITS else None
+
+        def rows_at(s):
+            bh, rest = divmod(s, 4)
+            return (bh, rest - 2) if 0 <= s < UNITS and rest >= 2 else None
 
         eps_transposes(0)
+        unit_sigma(0)
         for s in range(SLOTS):
-            last_pair = pair_at(s - 1)
-            piece = divmod(s - 2, 2) if 2 <= s < 2 + UNITS else None
+            regrouped = piece_at(s - REGROUP_LAG)
+            quantised = piece_at(s - QUANTISE_LAG)
+            multiplied = rows_at(s - QUANTISE_LAG)
+            normalised = rows_at(s - QUANTISE_LAG - 1)
+            if s + 1 < UNITS:
+                unit_sigma(s + 1)
             if s < UNITS:
-                sig = unit_sigma(s)
-            if last_pair is not None:
-                softmax_min(*last_pair)
-                softmax_exp(*last_pair)
-            if s < UNITS:
-                noise = unit_noise(s, sig)
+                noise = unit_noise(s)
+            if normalised is not None:
+                softmax_min(*normalised)
+                softmax_exp(*normalised)
             if EARLY - 1 + s < len(operands):
                 operand_quantise(EARLY - 1 + s)
             if s == C2_SLOT + 1:
                 nc.vector.tensor_copy(out=c2_all[:], in_=c2_bank[:])
-            if 3 <= s < 3 + UNITS:
-                j, p = divmod(s - 3, 2)
-                quantise(nc, z_groupeds[(j, p)], z_codes[:, 2 * j + p], z_scales[:, 2 * j + p])
-            if piece is not None:
-                z_back(piece[0], piece[1], 0)
+            if quantised is not None:
+                quantise_z(*quantised)
             if s < UNITS:
                 unit_z(s, noise)
-            if last_pair is not None:
-                softmax_norm(*last_pair)
-            if pair_at(s) is not None:
-                distances(*pair_at(s))
-            if piece is not None:
-                regroup(*piece)
-                z_back(piece[0], piece[1], 1)
-                store_z(*piece)
+            if regrouped is not None:
+                regroup(*regrouped)
+            if normalised is not None:
+                softmax_norm(*normalised)
+            if quantised is not None:
+                store_z(*quantised)
+            if s + 1 < UNITS:
+                eps_transposes(s + 1)
             if EARLY + s < len(operands):
                 operand_transposes(EARLY + s)
             if s == C2_SLOT:
                 c2_bank = psum_tr.tile([P, K], F32, tag="tr")
                 nc.tensor.matmul(c2_bank[:], lhsT=ones[:], rhs=c2_part[:], start=True, stop=True)
-            if s + 1 < UNITS:
-                eps_transposes(s + 1)
+            if multiplied is not None:
+                distances(*multiplied)

@@ -309,9 +309,7 @@ def tile_latent_pa_kernel(
         def regroup(j, p):
             z_view = z32s[j][:, :, p * PIECE : (p + 1) * PIECE].rearrange("p t b -> p b t")
             z_grouped = three.tile([P, 2, PIECE, 4], BF16, tag="z_grouped", align_bytes=64)
-            nc.gpsimd.tensor_scalar(
-                out=z_grouped[:, 0, :, :], in0=z_view, scalar1=1.0, scalar2=0.0, op0=ALU.mult, op1=ALU.add
-            )
+            nc.vector.tensor_copy(out=z_grouped[:, 0, :, :], in_=z_view)
             nc.scalar.activation(out=z_grouped[:, 1, :, :], in_=z_view, func=ACT.Square)
             z_groupeds[(j, p)] = z_grouped
 

@@ -307,10 +307,12 @@ def tile_latent_pa_kernel(
                 )
 
         def regroup(j, p):
-            z_view = z32s[j][:, :, p * PIECE : (p + 1) * PIECE].rearrange("p t b -> p b t")
+            z_view = z32s[j][:, :, p * PIECE : (p + 1) * PIECE].rearrange("p t (c i) -> p c t i", i=4)
             z_grouped = three.tile([P, 2, PIECE, 4], BF16, tag="z_grouped", align_bytes=64)
-            nc.vector.tensor_copy(out=z_grouped[:, 0, :, :], in_=z_view)
-            nc.scalar.activation(out=z_grouped[:, 1, :, :], in_=z_view, func=ACT.Square)
+            nc.vector.tensor_copy(out=z_grouped[:, 0, :, :].rearrange("p (c i) t -> p c t i", i=4), in_=z_view)
+            nc.scalar.activation(
+                out=z_grouped[:, 1, :, :].rearrange("p (c i) t -> p c t i", i=4), in_=z_view, func=ACT.Square
+            )
             z_groupeds[(j, p)] = z_grouped
 
         def quantise_z(j, p):

@@ -17,10 +17,12 @@ HALF = 512
 PIECE = 256
 UNITS = 8
 EARLY = 4
-C2_SLOT = 2
-REGROUP_LAG = 2
-QUANTISE_LAG = REGROUP_LAG + 1
-SLOTS = UNITS + QUANTISE_LAG + 1
+C2_SLOT = 3
+LAST_GROUP = 3
+SQUARE_LAG = 1
+QUANTISE_LAG = 2
+STORE_LAG = 3
+SLOTS = UNITS + STORE_LAG + 1
 
 FLOPS = 2 * B * H * H * 2 + 2 * B * K * H * 2
 
@@ -242,6 +244,7 @@ def tile_latent_pa_kernel(
             quantise(nc, minv_grouped, minv_codes[:], minv_scales[:])
 
         two = ctx.enter_context(tc.tile_pool(name="two", bufs=2, reuse_waits="tile"))
+        six = ctx.enter_context(tc.tile_pool(name="six", bufs=6, reuse_waits="tile"))
         three = ctx.enter_context(tc.tile_pool(name="three", bufs=3, reuse_waits="tile"))
         eps_words = eps_nat[:].bitcast(F32)
         eps_banks = {}
@@ -306,14 +309,28 @@ def tile_latent_pa_kernel(
                     op1=ALU.add,
                 )
 
-        def regroup(j, p):
-            z_view = z32s[j][:, :, p * PIECE : (p + 1) * PIECE].rearrange("p t (c i) -> p c t i", i=4)
-            z_grouped = three.tile([P, 2, PIECE, 4], BF16, tag="z_grouped", align_bytes=64)
-            nc.vector.tensor_copy(out=z_grouped[:, 0, :, :].rearrange("p (c i) t -> p c t i", i=4), in_=z_view)
+        def z_tile(j, p):
+            if (j, p) not in z_groupeds:
+                z_grouped = three.tile([P, 2, PIECE, 4], BF16, tag="z_grouped", align_bytes=64)
+                z_groupeds[(j, p)] = z_grouped
+            return z_groupeds[(j, p)]
+
+        def in_runs(z_view):
+            return z_view.rearrange("p (c i) t -> p c t i", i=4)
+
+        def regroup_z(j, p):
+            z_view = z32s[j][:, :, p * PIECE : (p + 1) * PIECE].rearrange("p t b -> p b t")
+            grouped = z_tile(j, p)[:, 0, :, :]
+            if j < LAST_GROUP:
+                nc.gpsimd.tensor_scalar(out=grouped, in0=z_view, scalar1=1.0, scalar2=0.0, op0=ALU.mult, op1=ALU.add)
+            else:
+                nc.vector.tensor_copy(out=in_runs(grouped), in_=in_runs(z_view))
+
+        def regroup_square(j, p):
+            z_view = z32s[j][:, :, p * PIECE : (p + 1) * PIECE].rearrange("p t b -> p b t")
             nc.scalar.activation(
-                out=z_grouped[:, 1, :, :].rearrange("p (c i) t -> p c t i", i=4), in_=z_view, func=ACT.Square
+                out=in_runs(z_tile(j, p)[:, 1, :, :]), in_=in_runs(z_view), func=ACT.Square
             )
-            z_groupeds[(j, p)] = z_grouped
 
         def quantise_z(j, p):
             quantise(nc, z_groupeds[(j, p)], z_codes[:, 2 * j + p], z_scales[:, 2 * j + p])
@@ -326,10 +343,12 @@ def tile_latent_pa_kernel(
                 back = psum_tr.tile([P, 4, P], F32, tag="tr")
                 for t in range(4):
                     nc.tensor.transpose(back[:, t, :], z32s[j][:, t, first : first + P], ident[:])
-                nc.scalar.copy(
-                    out=z_out[:, i, :].rearrange("p (u q e) -> p u q e", u=2, e=2),
-                    in_=back[:].rearrange("p (u e) q -> p u q e", e=2),
-                )
+                ordered = z_out[:, i, :].rearrange("p (u q e) -> p u q e", u=2, e=2)
+                bank = back[:].rearrange("p (u e) q -> p u q e", e=2)
+                if (p, i) == (1, 1):
+                    nc.vector.tensor_copy(out=ordered, in_=bank)
+                else:
+                    nc.scalar.copy(out=ordered, in_=bank)
             row0 = HALF * bh + PIECE * p
             nc.sync.dma_start(
                 out=out_0[row0 : row0 + PIECE, HALF * g : HALF * g + HALF].rearrange("(i r) h -> r i h", r=P),
@@ -357,7 +376,7 @@ def tile_latent_pa_kernel(
         def softmax_min(bh, p):
             ds = []
             for i in range(2):
-                d = two.tile([P, K], F32, tag="d")
+                d = six.tile([P, K], F32, tag="d")
                 nc.vector.tensor_tensor(out=d[:], in0=d_accs[(bh, p, i)][:], in1=c2_all[:], op=ALU.add)
                 ds.append(d)
             d_mins = []
@@ -369,29 +388,25 @@ def tile_latent_pa_kernel(
 
         def softmax_exp(bh, p):
             ds, d_mins = soft[(bh, p)]
-            weights = []
             totals = []
             for i in range(2):
-                weight = two.tile([P, K], F32, tag="weight")
                 total = two.tile([P, 1], F32, tag="total")
                 nc.scalar.activation(
-                    out=weight[:], in_=ds[i][:], func=ACT.Exp, bias=d_mins[i][:], scale=-1.0, accum_out=total[:]
+                    out=ds[i][:], in_=ds[i][:], func=ACT.Exp, bias=d_mins[i][:], scale=-1.0, accum_out=total[:]
                 )
-                weights.append(weight)
                 totals.append(total)
-            soft[(bh, p)] = (weights, totals)
+            soft[(bh, p)] = (ds, totals)
 
         def softmax_norm(bh, p):
             weights, totals = soft[(bh, p)]
             for i in range(2):
                 inv_total = two.tile([P, 1], F32, tag="inv_total")
                 nc.vector.reciprocal(out=inv_total[:], in_=totals[i][:])
-                att = two.tile([P, K], F32, tag="att")
                 nc.gpsimd.tensor_scalar(
-                    out=att[:], in0=weights[i][:], scalar1=inv_total[:], scalar2=0.0, op0=ALU.mult, op1=ALU.add
+                    out=weights[i][:], in0=weights[i][:], scalar1=inv_total[:], scalar2=0.0, op0=ALU.mult, op1=ALU.add
                 )
                 row0 = HALF * bh + PIECE * p + i * P
-                nc.sync.dma_start(out=out_1[row0 : row0 + P, :], in_=att[:])
+                nc.sync.dma_start(out=out_1[row0 : row0 + P, :], in_=weights[i][:])
 
         def piece_at(s):
             return divmod(s, 2) if 0 <= s < UNITS else None
@@ -403,37 +418,40 @@ def tile_latent_pa_kernel(
         eps_transposes(0)
         unit_sigma(0)
         for s in range(SLOTS):
-            regrouped = piece_at(s - REGROUP_LAG)
+            squared = piece_at(s - SQUARE_LAG)
             quantised = piece_at(s - QUANTISE_LAG)
-            multiplied = rows_at(s - QUANTISE_LAG)
-            normalised = rows_at(s - QUANTISE_LAG - 1)
-            if s + 1 < UNITS:
-                unit_sigma(s + 1)
-            if s < UNITS:
-                noise = unit_noise(s)
-            if normalised is not None:
-                softmax_min(*normalised)
-                softmax_exp(*normalised)
-            if EARLY - 1 + s < len(operands):
-                operand_quantise(EARLY - 1 + s)
+            stored = piece_at(s - STORE_LAG)
+            multiplied = rows_at(s - STORE_LAG)
+            normalised = rows_at(s - STORE_LAG - 1)
             if s == C2_SLOT + 1:
                 nc.vector.tensor_copy(out=c2_all[:], in_=c2_bank[:])
-            if quantised is not None:
-                quantise_z(*quantised)
-            if s < UNITS:
-                unit_z(s, noise)
-            if regrouped is not None:
-                regroup(*regrouped)
             if normalised is not None:
-                softmax_norm(*normalised)
-            if quantised is not None:
-                store_z(*quantised)
-            if s + 1 < UNITS:
-                eps_transposes(s + 1)
-            if EARLY + s < len(operands):
-                operand_transposes(EARLY + s)
+                softmax_min(*normalised)
+            if EARLY - 1 + s < len(operands):
+                operand_quantise(EARLY - 1 + s)
             if s == C2_SLOT:
                 c2_bank = psum_tr.tile([P, K], F32, tag="tr")
                 nc.tensor.matmul(c2_bank[:], lhsT=ones[:], rhs=c2_part[:], start=True, stop=True)
+            if s + 1 < UNITS:
+                unit_sigma(s + 1)
+            if EARLY + s < len(operands):
+                operand_transposes(EARLY + s)
+            if quantised is not None:
+                regroup_z(*quantised)
+            if normalised is not None:
+                softmax_exp(*normalised)
+            if s < UNITS:
+                noise = unit_noise(s)
+                unit_z(s, noise)
+            if stored is not None:
+                store_z(*stored)
+            if normalised is not None:
+                softmax_norm(*normalised)
+            if quantised is not None:
+                quantise_z(*quantised)
             if multiplied is not None:
                 distances(*multiplied)
+            if s + 1 < UNITS:
+                eps_transposes(s + 1)
+            if squared is not None:
+                regroup_square(*squared)

@@ -18,11 +18,8 @@ PIECE = 256
 UNITS = 8
 EARLY = 4
 C2_SLOT = 3
-LAST_GROUP = 3
-SQUARE_LAG = 1
-QUANTISE_LAG = 2
-STORE_LAG = 3
-SLOTS = UNITS + STORE_LAG + 1
+LAST_GROUP = 4
+SLOTS = UNITS + 6
 
 FLOPS = 2 * B * H * H * 2 + 2 * B * K * H * 2
 
@@ -345,10 +342,7 @@ def tile_latent_pa_kernel(
                     nc.tensor.transpose(back[:, t, :], z32s[j][:, t, first : first + P], ident[:])
                 ordered = z_out[:, i, :].rearrange("p (u q e) -> p u q e", u=2, e=2)
                 bank = back[:].rearrange("p (u e) q -> p u q e", e=2)
-                if (p, i) == (1, 1):
-                    nc.vector.tensor_copy(out=ordered, in_=bank)
-                else:
-                    nc.scalar.copy(out=ordered, in_=bank)
+                nc.scalar.copy(out=ordered, in_=bank)
             row0 = HALF * bh + PIECE * p
             nc.sync.dma_start(
                 out=out_0[row0 : row0 + PIECE, HALF * g : HALF * g + HALF].rearrange("(i r) h -> r i h", r=P),
@@ -402,8 +396,8 @@ def tile_latent_pa_kernel(
             for i in range(2):
                 inv_total = two.tile([P, 1], F32, tag="inv_total")
                 nc.vector.reciprocal(out=inv_total[:], in_=totals[i][:])
-                nc.gpsimd.tensor_scalar(
-                    out=weights[i][:], in0=weights[i][:], scalar1=inv_total[:], scalar2=0.0, op0=ALU.mult, op1=ALU.add
+                nc.vector.tensor_scalar(
+                    out=weights[i][:], in0=weights[i][:], scalar1=inv_total[:], scalar2=None, op0=ALU.mult
                 )
                 row0 = HALF * bh + PIECE * p + i * P
                 nc.sync.dma_start(out=out_1[row0 : row0 + P, :], in_=weights[i][:])
@@ -418,40 +412,36 @@ def tile_latent_pa_kernel(
         eps_transposes(0)
         unit_sigma(0)
         for s in range(SLOTS):
-            squared = piece_at(s - SQUARE_LAG)
-            quantised = piece_at(s - QUANTISE_LAG)
-            stored = piece_at(s - STORE_LAG)
-            multiplied = rows_at(s - STORE_LAG)
-            normalised = rows_at(s - STORE_LAG - 1)
-            if s == C2_SLOT + 1:
-                nc.vector.tensor_copy(out=c2_all[:], in_=c2_bank[:])
-            if normalised is not None:
-                softmax_min(*normalised)
-            if EARLY - 1 + s < len(operands):
-                operand_quantise(EARLY - 1 + s)
+            if rows_at(s - 6) is not None:
+                softmax_norm(*rows_at(s - 6))
             if s == C2_SLOT:
                 c2_bank = psum_tr.tile([P, K], F32, tag="tr")
                 nc.tensor.matmul(c2_bank[:], lhsT=ones[:], rhs=c2_part[:], start=True, stop=True)
+            if s < UNITS:
+                noise = unit_noise(s)
+            if EARLY - 1 + s < len(operands):
+                operand_quantise(EARLY - 1 + s)
+            if s < UNITS:
+                unit_z(s, noise)
+            if piece_at(s - 2) is not None:
+                quantise_z(*piece_at(s - 2))
+            if s == C2_SLOT + 1:
+                nc.vector.tensor_copy(out=c2_all[:], in_=c2_bank[:])
+            if rows_at(s - 4) is not None:
+                distances(*rows_at(s - 4))
+            if rows_at(s - 5) is not None:
+                softmax_exp(*rows_at(s - 5))
             if s + 1 < UNITS:
                 unit_sigma(s + 1)
             if EARLY + s < len(operands):
                 operand_transposes(EARLY + s)
-            if quantised is not None:
-                regroup_z(*quantised)
-            if normalised is not None:
-                softmax_exp(*normalised)
-            if s < UNITS:
-                noise = unit_noise(s)
-                unit_z(s, noise)
-            if stored is not None:
-                store_z(*stored)
-            if normalised is not None:
-                softmax_norm(*normalised)
-            if quantised is not None:
-                quantise_z(*quantised)
-            if multiplied is not None:
-                distances(*multiplied)
+            if rows_at(s - 4) is not None:
+                softmax_min(*rows_at(s - 4))
             if s + 1 < UNITS:
                 eps_transposes(s + 1)
-            if squared is not None:
-                regroup_square(*squared)
+            if piece_at(s - 1) is not None:
+                regroup_z(*piece_at(s - 1))
+            if piece_at(s - 1) is not None:
+                regroup_square(*piece_at(s - 1))
+            if piece_at(s - 3) is not None:
+                store_z(*piece_at(s - 3))

from contextlib import ExitStack

import concourse.mybir as mybir
from concourse.masks import make_identity

F32 = mybir.dt.float32
BF16 = mybir.dt.bfloat16
U32 = mybir.dt.uint32
U8 = mybir.dt.uint8
FP8X4 = mybir.dt.float8_e4m3fn_x4
ACT = mybir.ActivationFunctionType
ALU = mybir.AluOpType

P = 128
B, H, K = 1024, 1024, 512
HALF = 512
PIECE = 256
UNITS = 8
EARLY = 4
C2_SLOT = 3
LAST_GROUP = 4
SLOTS = UNITS + 6

FLOPS = 2 * B * H * H * 2 + 2 * B * K * H * 2


def quantise(nc, grouped, codes, scales):
    nc.vector.quantize_mx(
        out=codes.rearrange("p g c -> p (g c)").bitcast(FP8X4),
        scales=scales.rearrange("p g c -> p (g c)"),
        in_=grouped[:].rearrange("p g c t -> p (g c t)"),
    )


def transpose_rows(nc, psum_tr, stage, ident, rows):
    words = rows.bitcast(F32)
    grouped = stage.tile([P, 2, HALF, 4], BF16, tag="grouped", align_bytes=64)
    grouped_words = grouped[:].bitcast(F32)
    for i in range(4):
        bank = psum_tr.tile([P, 4, P], F32, tag="tr")
        for j in range(4):
            nc.tensor.transpose(bank[:, j, :], words[:, i, j * P : (j + 1) * P], ident[:])
        nc.scalar.copy(
            out=grouped_words[:, :, i * P : (i + 1) * P, :],
            in_=bank[:].rearrange("p (g u) r -> p g r u", g=2),
        )
    return grouped


def project(nc, bank, w_codes, w_scales, row_tile, x_codes, x_scales, bh):
    half, i = divmod(row_tile, 4)
    cols = slice(i * P, (i + 1) * P)
    for g in range(2):
        nc.tensor.matmul_mx(
            out=bank[:],
            lhsT=w_codes[:, half, g, cols].bitcast(FP8X4),
            lhsT_scale=w_scales[:, half, g, cols],
            rhs=x_codes[:, bh, g, :].bitcast(FP8X4),
            rhs_scale=x_scales[:, bh, g, :],
            start=(g == 0),
            stop=(g == 1),
        )


def tile_latent_pa_kernel(
    tc, encoder_final_state, W_mu, b_mu, W_ls, b_ls, mu_c, log_sigma_sq_c, eps_z, out_0, out_1
):
    nc = tc.nc
    with ExitStack() as ctx:
        ctx.enter_context(tc.manual_schedule())
        const = ctx.enter_context(tc.tile_pool(name="const", bufs=1))
        raw = ctx.enter_context(tc.tile_pool(name="raw", bufs=1))
        keep = ctx.enter_context(tc.tile_pool(name="keep", bufs=1))
        stage = ctx.enter_context(tc.tile_pool(name="stage", bufs=3))
        psum_tr = ctx.enter_context(tc.psum_pool(name="psum_tr", bufs=4))
        psum_mm = ctx.enter_context(tc.psum_pool(name="psum_mm", bufs=4))

        ident = const.tile([P, P], F32)
        make_identity(nc, ident[:])
        ones = const.tile([P, P], F32)
        nc.vector.memset(ones[:], 1.0)
        bias_rows = const.tile([P, P], F32)
        nc.vector.memset(bias_rows[:], 0.0)
        bias = const.tile([P, 16], F32)
        c2_part = const.tile([P, K], F32)
        c2_all = const.tile([P, K], F32)

        x_nat = raw.tile([P, 8, H], BF16)
        wls_nat = raw.tile([P, 8, H], BF16)
        wmu_nat = raw.tile([P, 8, H], BF16)
        eps_nat = raw.tile([P, 8, H], BF16)

        x_codes = keep.tile([P, 2, 2, HALF], U32, align_bytes=64)
        x_scales = keep.tile([P, 2, 2, HALF], U8, align_bytes=64)
        wls_codes = keep.tile([P, 2, 2, HALF], U32, align_bytes=64)
        wls_scales = keep.tile([P, 2, 2, HALF], U8, align_bytes=64)
        wmu_codes = keep.tile([P, 2, 2, HALF], U32, align_bytes=64)
        wmu_scales = keep.tile([P, 2, 2, HALF], U8, align_bytes=64)
        inv_codes = keep.tile([P, 2, K], U32, align_bytes=64)
        inv_scales = keep.tile([P, 2, K], U8, align_bytes=64)
        minv_codes = keep.tile([P, 2, K], U32, align_bytes=64)
        minv_scales = keep.tile([P, 2, K], U8, align_bytes=64)
        z_codes = keep.tile([P, 8, 2, PIECE], U32, align_bytes=64)
        z_scales = keep.tile([P, 8, 2, PIECE], U8, align_bytes=64)

        def load_rows(nat, src, half):
            nc.sync.dma_start(
                out=nat[:, 4 * half : 4 * half + 4, :],
                in_=src[HALF * half : HALF * half + HALF, :].rearrange("(t r) h -> r t h", r=P),
            )

        def load_weight(nat, src, half):
            nc.sync.dma_start(
                out=nat[:, 4 * half : 4 * half + 4, :].rearrange("q (a e) h -> q a (e h)", e=2),
                in_=src[HALF * half : HALF * half + HALF, :].rearrange("(a q e) h -> q a (e h)", q=P, e=2),
            )

        nc.sync.dma_start(out=bias_rows[0:4, :].bitcast(BF16), in_=b_mu.rearrange("(a w) -> a w", a=4))
        nc.sync.dma_start(out=bias_rows[4:8, :].bitcast(BF16), in_=b_ls.rearrange("(a w) -> a w", a=4))
        with tc.tile_pool(name="cl_tmp", bufs=3) as cl_tmp, tc.tile_pool(name="cl_keep", bufs=1) as cl_keep:
            ls_nat = cl_keep.tile([P, 4, H], BF16)
            mu_nat = cl_keep.tile([P, 4, H], BF16)
            for ch in range(2):
                for nat, src in ((ls_nat, log_sigma_sq_c), (mu_nat, mu_c)):
                    nc.sync.dma_start(
                        out=nat[:, 2 * ch : 2 * ch + 2, :],
                        in_=src[PIECE * ch : PIECE * ch + PIECE, :].rearrange("(t r) h -> r t h", r=P),
                    )
            load_rows(x_nat, encoder_final_state, 0)
            load_weight(wls_nat, W_ls, 0)
            load_weight(wmu_nat, W_mu, 0)
            load_weight(wls_nat, W_ls, 1)
            load_rows(eps_nat, eps_z, 0)
            load_weight(wmu_nat, W_mu, 1)
            load_rows(x_nat, encoder_final_state, 1)
            load_rows(eps_nat, eps_z, 1)

            bias_bank = psum_tr.tile([P, P], F32, tag="tr")
            nc.tensor.transpose(bias_bank[:], bias_rows[:], ident[:])
            nc.vector.tensor_copy(out=bias[:, 0:8], in_=bias_bank[:, 0:4].bitcast(BF16))
            nc.vector.tensor_scalar(
                out=bias[:, 8:16], in0=bias_bank[:, 4:8].bitcast(BF16), scalar1=0.5, scalar2=None, op0=ALU.mult
            )

            ls_words = ls_nat[:].bitcast(F32)
            mu_words = mu_nat[:].bitcast(F32)
            inv_grouped = cl_keep.tile([P, 2, K, 4], BF16, align_bytes=64)
            minv_grouped = cl_keep.tile([P, 2, K, 4], BF16, align_bytes=64)
            prod = cl_keep.tile([P, 2, 4, K], F32)
            items = [(ch, g) for ch in range(2) for g in range(2)]
            mu_views = []
            inv32s = []
            for ch, g in items:
                ls_bank = psum_tr.tile([P, 2, PIECE], F32, tag="tr")
                mu_bank = psum_mm.tile([P, 2, PIECE], F32, tag="mm")
                for bank, words in ((ls_bank, ls_words), (mu_bank, mu_words)):
                    for u in range(2):
                        for j in range(2):
                            nc.tensor.transpose(
                                bank[:, u, j * P : (j + 1) * P],
                                words[:, 2 * ch + j, (2 * g + u) * P : (2 * g + u + 1) * P],
                                ident[:],
                            )
                mu_views.append(mu_bank[:].bitcast(BF16).rearrange("p u (c e) -> p c u e", e=2))
                inv32 = cl_tmp.tile([P, PIECE, 2, 2], F32)
                nc.scalar.activation(
                    out=inv32[:],
                    in_=ls_bank[:].bitcast(BF16).rearrange("p u (c e) -> p c u e", e=2),
                    func=ACT.Exp,
                    scale=-1.0,
                )
                inv32s.append(inv32)
            minv32s = []

            def scaled_means(n):
                ch, g = items[n]
                cols = slice(PIECE * ch, PIECE * ch + PIECE)
                nc.gpsimd.tensor_scalar(
                    out=inv_grouped[:, g, cols, :].rearrange("p c (u e) -> p c u e", e=2),
                    in0=inv32s[n][:],
                    scalar1=1.0,
                    scalar2=0.0,
                    op0=ALU.mult,
                    op1=ALU.add,
                )
                minv32 = cl_tmp.tile([P, PIECE, 2, 2], F32)
                nc.vector.tensor_tensor(out=minv32[:], in0=mu_views[n], in1=inv32s[n][:], op=ALU.mult)
                nc.gpsimd.tensor_scalar(
                    out=minv_grouped[:, g, cols, :].rearrange("p c (u e) -> p c u e", e=2),
                    in0=minv32[:],
                    scalar1=-2.0,
                    scalar2=0.0,
                    op0=ALU.mult,
                    op1=ALU.add,
                )
                minv32s.append(minv32)

            def c2_terms(n):
                ch, g = items[n]
                cols = slice(PIECE * ch, PIECE * ch + PIECE)
                nc.vector.tensor_tensor(
                    out=prod[:, g, :, cols].rearrange("p (u e) c -> p c u e", e=2),
                    in0=mu_views[n],
                    in1=minv32s[n][:],
                    op=ALU.mult,
                )

            scaled_means(0)
            for n in range(1, len(items)):
                scaled_means(n)
                c2_terms(n - 1)
            c2_terms(len(items) - 1)
            nc.gpsimd.tensor_tensor(out=prod[:, :, 0, :], in0=prod[:, :, 0, :], in1=prod[:, :, 1, :], op=ALU.add)
            nc.gpsimd.tensor_tensor(out=prod[:, :, 2, :], in0=prod[:, :, 2, :], in1=prod[:, :, 3, :], op=ALU.add)
            nc.gpsimd.tensor_tensor(out=prod[:, :, 0, :], in0=prod[:, :, 0, :], in1=prod[:, :, 2, :], op=ALU.add)
            nc.gpsimd.tensor_tensor(out=c2_part[:], in0=prod[:, 0, 0, :], in1=prod[:, 1, 0, :], op=ALU.add)

            operands = [
                (x_nat, x_codes, x_scales, 0),
                (wls_nat, wls_codes, wls_scales, 0),
                (wmu_nat, wmu_codes, wmu_scales, 0),
                (wls_nat, wls_codes, wls_scales, 1),
                (wmu_nat, wmu_codes, wmu_scales, 1),
                (x_nat, x_codes, x_scales, 1),
            ]
            grouped_of = {}

            def operand_transposes(n):
                nat, codes, scales, half = operands[n]
                grouped_of[n] = transpose_rows(nc, psum_tr, stage, ident, nat[:, 4 * half : 4 * half + 4, :])

            def operand_quantise(n):
                nat, codes, scales, half = operands[n]
                quantise(nc, grouped_of[n], codes[:, half], scales[:, half])

            for n in range(EARLY):
                operand_transposes(n)
                if n > 0:
                    operand_quantise(n - 1)
            quantise(nc, inv_grouped, inv_codes[:], inv_scales[:])
            quantise(nc, minv_grouped, minv_codes[:], minv_scales[:])

        two = ctx.enter_context(tc.tile_pool(name="two", bufs=2, reuse_waits="tile"))
        six = ctx.enter_context(tc.tile_pool(name="six", bufs=6, reuse_waits="tile"))
        three = ctx.enter_context(tc.tile_pool(name="three", bufs=3, reuse_waits="tile"))
        eps_words = eps_nat[:].bitcast(F32)
        eps_banks = {}
        sigs = {}
        z32s = {}
        z_groupeds = {}
        z_outs = {}
        d_accs = {}
        soft = {}

        def eps_transposes(s):
            bh, a = divmod(s, 4)
            eps_bank = psum_tr.tile([P, HALF], F32, tag="tr")
            for i in range(4):
                nc.tensor.transpose(
                    eps_bank[:, i * P : (i + 1) * P], eps_words[:, 4 * bh + i, a * P : (a + 1) * P], ident[:]
                )
            eps_banks[s] = eps_bank

        def unit_sigma(s):
            bh, a = divmod(s, 4)
            sig = three.tile([P, 2, HALF], F32, tag="sig")
            for e in range(2):
                row_tile = 2 * a + e
                ls_acc = psum_mm.tile([P, HALF], F32, tag="mm")
                project(nc, ls_acc, wls_codes, wls_scales, row_tile, x_codes, x_scales, bh)
                nc.scalar.activation(
                    out=sig[:, e, :],
                    in_=ls_acc[:],
                    func=ACT.Exp,
                    bias=bias[:, 8 + row_tile : 9 + row_tile],
                    scale=0.5,
                )
            sigs[s] = sig

        def unit_noise(s):
            noise = two.tile([P, HALF, 2], F32, tag="noise")
            nc.vector.tensor_tensor(
                out=noise[:],
                in0=sigs[s][:].rearrange("p e b -> p b e"),
                in1=eps_banks[s][:].bitcast(BF16).rearrange("p (b e) -> p b e", e=2),
                op=ALU.mult,
            )
            return noise

        def unit_z(s, noise):
            bh, a = divmod(s, 4)
            u = a % 2
            if u == 0:
                z32 = three.tile([P, 4, HALF], F32, tag="z32")
                z32s[s // 2] = z32
            for e in range(2):
                row_tile = 2 * a + e
                mu_acc = psum_mm.tile([P, HALF], F32, tag="mm")
                project(nc, mu_acc, wmu_codes, wmu_scales, row_tile, x_codes, x_scales, bh)
                nc.vector.scalar_tensor_tensor(
                    out=z32s[s // 2][:, 2 * u + e, :],
                    in0=mu_acc[:],
                    scalar=bias[:, row_tile : row_tile + 1],
                    in1=noise[:, :, e],
                    op0=ALU.add,
                    op1=ALU.add,
                )

        def z_tile(j, p):
            if (j, p) not in z_groupeds:
                z_grouped = three.tile([P, 2, PIECE, 4], BF16, tag="z_grouped", align_bytes=64)
                z_groupeds[(j, p)] = z_grouped
            return z_groupeds[(j, p)]

        def in_runs(z_view):
            return z_view.rearrange("p (c i) t -> p c t i", i=4)

        def regroup_z(j, p):
            z_view = z32s[j][:, :, p * PIECE : (p + 1) * PIECE].rearrange("p t b -> p b t")
            grouped = z_tile(j, p)[:, 0, :, :]
            if j < LAST_GROUP:
                nc.gpsimd.tensor_scalar(out=grouped, in0=z_view, scalar1=1.0, scalar2=0.0, op0=ALU.mult, op1=ALU.add)
            else:
                nc.vector.tensor_copy(out=in_runs(grouped), in_=in_runs(z_view))

        def regroup_square(j, p):
            z_view = z32s[j][:, :, p * PIECE : (p + 1) * PIECE].rearrange("p t b -> p b t")
            nc.scalar.activation(
                out=in_runs(z_tile(j, p)[:, 1, :, :]), in_=in_runs(z_view), func=ACT.Square
            )

        def quantise_z(j, p):
            quantise(nc, z_groupeds[(j, p)], z_codes[:, 2 * j + p], z_scales[:, 2 * j + p])

        def store_z(j, p):
            bh, g = divmod(j, 2)
            z_out = three.tile([P, 2, HALF], F32, tag="z_out")
            for i in range(2):
                first = (2 * p + i) * P
                back = psum_tr.tile([P, 4, P], F32, tag="tr")
                for t in range(4):
                    nc.tensor.transpose(back[:, t, :], z32s[j][:, t, first : first + P], ident[:])
                ordered = z_out[:, i, :].rearrange("p (u q e) -> p u q e", u=2, e=2)
                bank = back[:].rearrange("p (u e) q -> p u q e", e=2)
                nc.scalar.copy(out=ordered, in_=bank)
            row0 = HALF * bh + PIECE * p
            nc.sync.dma_start(
                out=out_0[row0 : row0 + PIECE, HALF * g : HALF * g + HALF].rearrange("(i r) h -> r i h", r=P),
                in_=z_out[:],
            )

        def distances(bh, p):
            for i in range(2):
                cols = slice(i * P, (i + 1) * P)
                d_acc = psum_mm.tile([P, K], F32, tag="mm")
                for g in range(2):
                    piece = 2 * (2 * bh + g) + p
                    for kind, (c_codes, c_scales) in enumerate(((minv_codes, minv_scales), (inv_codes, inv_scales))):
                        nc.tensor.matmul_mx(
                            out=d_acc[:],
                            lhsT=z_codes[:, piece, kind, cols].bitcast(FP8X4),
                            lhsT_scale=z_scales[:, piece, kind, cols],
                            rhs=c_codes[:, g, :].bitcast(FP8X4),
                            rhs_scale=c_scales[:, g, :],
                            start=(g == 0 and kind == 0),
                            stop=(g == 1 and kind == 1),
                        )
                d_accs[(bh, p, i)] = d_acc

        def softmax_min(bh, p):
            ds = []
            for i in range(2):
                d = six.tile([P, K], F32, tag="d")
                nc.vector.tensor_tensor(out=d[:], in0=d_accs[(bh, p, i)][:], in1=c2_all[:], op=ALU.add)
                ds.append(d)
            d_mins = []
            for i in range(2):
                d_min = two.tile([P, 1], F32, tag="d_min")
                nc.vector.tensor_reduce(out=d_min[:], in_=ds[i][:], axis=mybir.AxisListType.X, op=ALU.min)
                d_mins.append(d_min)
            soft[(bh, p)] = (ds, d_mins)

        def softmax_exp(bh, p):
            ds, d_mins = soft[(bh, p)]
            totals = []
            for i in range(2):
                total = two.tile([P, 1], F32, tag="total")
                nc.scalar.activation(
                    out=ds[i][:], in_=ds[i][:], func=ACT.Exp, bias=d_mins[i][:], scale=-1.0, accum_out=total[:]
                )
                totals.append(total)
            soft[(bh, p)] = (ds, totals)

        def softmax_norm(bh, p):
            weights, totals = soft[(bh, p)]
            for i in range(2):
                inv_total = two.tile([P, 1], F32, tag="inv_total")
                nc.vector.reciprocal(out=inv_total[:], in_=totals[i][:])
                nc.vector.tensor_scalar(
                    out=weights[i][:], in0=weights[i][:], scalar1=inv_total[:], scalar2=None, op0=ALU.mult
                )
                row0 = HALF * bh + PIECE * p + i * P
                nc.sync.dma_start(out=out_1[row0 : row0 + P, :], in_=weights[i][:])

        def piece_at(s):
            return divmod(s, 2) if 0 <= s < UNITS else None

        def rows_at(s):
            bh, rest = divmod(s, 4)
            return (bh, rest - 2) if 0 <= s < UNITS and rest >= 2 else None

        eps_transposes(0)
        unit_sigma(0)
        for s in range(SLOTS):
            if rows_at(s - 6) is not None:
                softmax_norm(*rows_at(s - 6))
            if s == C2_SLOT:
                c2_bank = psum_tr.tile([P, K], F32, tag="tr")
                nc.tensor.matmul(c2_bank[:], lhsT=ones[:], rhs=c2_part[:], start=True, stop=True)
            if s < UNITS:
                noise = unit_noise(s)
            if EARLY - 1 + s < len(operands):
                operand_quantise(EARLY - 1 + s)
            if s < UNITS:
                unit_z(s, noise)
            if piece_at(s - 2) is not None:
                quantise_z(*piece_at(s - 2))
            if s == C2_SLOT + 1:
                nc.vector.tensor_copy(out=c2_all[:], in_=c2_bank[:])
            if rows_at(s - 4) is not None:
                distances(*rows_at(s - 4))
            if rows_at(s - 5) is not None:
                softmax_exp(*rows_at(s - 5))
            if s + 1 < UNITS:
                unit_sigma(s + 1)
            if EARLY + s < len(operands):
                operand_transposes(EARLY + s)
            if rows_at(s - 4) is not None:
                softmax_min(*rows_at(s - 4))
            if s + 1 < UNITS:
                eps_transposes(s + 1)
            if piece_at(s - 1) is not None:
                regroup_z(*piece_at(s - 1))
            if piece_at(s - 1) is not None:
                regroup_square(*piece_at(s - 1))
            if piece_at(s - 3) is not None:
                store_z(*piece_at(s - 3))
